import numpy as np
import ml_dtypes


def mxq(x, axis, fmt="e4m3"):
    dtype, down = {"e4m3": (ml_dtypes.float8_e4m3fn, 7), "e5m2": (ml_dtypes.float8_e5m2, 14)}[fmt]
    v = np.moveaxis(np.asarray(x, np.float32).astype(ml_dtypes.bfloat16).astype(np.float64), axis, -1)
    blocks = v.reshape(v.shape[:-1] + (-1, 32))
    amax = np.abs(blocks).max(-1, keepdims=True)
    byte = np.maximum(np.where(amax > 0, np.frexp(amax)[1] - 1 + 127, 0) - down, 1)
    scale = np.exp2(byte - 127.0)
    codes = (blocks / scale).astype(np.float32).astype(dtype).astype(np.float64)
    return np.moveaxis((codes * scale).reshape(v.shape), -1, axis)


WIDE = False


def mx_kscale(k):
    if not WIDE:
        return np.ones(k)
    levels = np.array([20, -20, 10, -10, 0])
    a = np.random.permutation(np.resize(levels, k // 512 * 4)).reshape(k // 512, 4)
    idx = np.arange(k)
    return np.exp2(a[idx // 512, idx % 128 // 32])


BF16 = ml_dtypes.bfloat16


def bf(x):
    return np.asarray(x, np.float32).astype(BF16)


def f64(x):
    return np.asarray(x).astype(np.float64)


B, S, D, K = 128, 8, 1024, 2048
T = B * S
GS = 4096.0


def setup_inputs():
    t = np.exp2(np.round(np.log2(mx_kscale(T)[::S]) / 2))[:, None, None]
    q = np.random.standard_normal((B, S, D))
    a = 0.3 * np.random.standard_normal((B, S, 1))
    p = np.random.standard_normal((B, S, D)) + a * q[:, -1:, :]
    W = bf(np.random.uniform(0.0, 1.0, (K, D)) * np.sqrt(12.0 / D))
    p0, q0 = bf(p), bf(q)
    g = np.random.standard_normal((B, K, S)) * np.exp2(np.random.randint(-12, 1, (B, 1, S))) * GS / (t * t)
    g = bf(g.reshape(B, S, K))
    pf, W2 = f64(p0), f64(W) * f64(W)
    ql = f64(q0)[:, -1, :]
    dot = ((pf * ql[:, None, :]) @ W2.T).transpose(0, 2, 1)
    np2 = ((pf * pf) @ W2.T).transpose(0, 2, 1)
    nq2 = (ql * ql) @ W2.T
    return {"p": bf(f64(p0) * t), "q": bf(f64(q0) * t), "W": W,
            "dot": np.ascontiguousarray(dot, dtype=np.float32),
            "np2": np.ascontiguousarray(np2, dtype=np.float32),
            "nq2": np.ascontiguousarray(nq2, dtype=np.float32),
            "grad_out": g}


def reference(p, q, W, dot, np2, nq2, grad_out):
    p, W = f64(p), f64(W)
    ql = f64(q)[:, -1, :]
    dot, np2, nq2 = f64(dot), f64(np2), f64(nq2)
    G = f64(grad_out).reshape(B, K, S)
    r = 1.0 / (np.sqrt(np2) * np.sqrt(nq2)[:, :, None] * D)
    g_dot = -G * r
    h = 0.5 * G * dot * r
    g_np2 = h / np2
    g_nq2 = h.sum(axis=2) / nq2
    a1 = mxq(g_dot.transpose(0, 2, 1).reshape(T, K), 0, "e5m2")
    a2 = mxq(g_np2.transpose(0, 2, 1).reshape(T, K), 0, "e5m2")
    x1 = mxq((p * ql[:, None, :]).reshape(T, D), 0, "e4m3")
    x2 = mxq((p * p).reshape(T, D), 0, "e4m3")
    gW2 = (a1.T @ x1) + (a2.T @ x2)
    gW2 = gW2 + g_nq2.T @ (ql * ql)
    return 2.0 * W * gW2

@@ -1,0 +1,234 @@
+from contextlib import ExitStack
+
+import concourse.mybir as mybir
+
+F32 = mybir.dt.float32
+BF16 = mybir.dt.bfloat16
+U32 = mybir.dt.uint32
+U8 = mybir.dt.uint8
+E4M3X4 = mybir.dt.float8_e4m3fn_x4
+E5M2X4 = mybir.dt.float8_e5m2_x4
+ACT = mybir.ActivationFunctionType
+ALU = mybir.AluOpType
+
+P = 128
+S = 8
+D = 1024
+K = 2048
+PACK = 4
+HALVES = S // PACK
+KT = 128
+TILES = 2
+KC = KT * TILES
+CHUNKS = K // KC
+CE = KC * S
+TE = KT * S
+DT = 512
+BANKS = D // DT
+
+FLOPS = 2 * (2 * P * S * K * D) + 2 * P * K * D
+BYTES = 2 * (P * S * D + P * D + K * D + P * S * K) + 4 * (2 * P * K * S + P * K + K * D)
+
+BANDS = ((0, 4, 32), (64, 2, 0), (96, 2, 96))
+
+
+def load_by_batch(nc, dst, src):
+    for first_batch, repeats, first_partition in BANDS:
+        rows = 16 * repeats
+        nc.sync.dma_start(
+            out=dst[first_partition : first_partition + rows, :],
+            in_=src[first_batch : first_batch + rows, :].rearrange("(u r) f -> r u f", r=16),
+        )
+
+
+def tile_mpl_v_kernel(tc, p, q, W, dot, np2, nq2, grad_out, out):
+    nc = tc.nc
+    p_flat = p.rearrange("b s d -> b (s d)")
+    g_flat = grad_out.rearrange("b s k -> b (s k)")
+    dot_flat = dot.rearrange("b k s -> b (k s)")
+    np2_flat = np2.rearrange("b k s -> b (k s)")
+    w_tiles = W.rearrange("(t r) d -> r t d", r=KT)
+
+    with ExitStack() as ctx:
+        ctx.enter_context(tc.manual_schedule())
+        keep = ctx.enter_context(tc.tile_pool(name="keep", bufs=1))
+        loads = ctx.enter_context(tc.tile_pool(name="loads", bufs=3))
+        work = ctx.enter_context(tc.tile_pool(name="work", bufs=2))
+        psum_mx = ctx.enter_context(tc.psum_pool(name="psum_mx", bufs=4))
+        psum_third = ctx.enter_context(tc.psum_pool(name="psum_third", bufs=4))
+
+        v2 = keep.tile([P, K], F32)
+        inq = keep.tile([P, K], F32)
+        ql = keep.tile([P, D], BF16)
+        ql2 = keep.tile([P, D], F32)
+        x_codes = keep.tile([P, 2, HALVES, D], U32, align_bytes=64)
+        x_scales = keep.tile([P, 2, HALVES, D], U8, align_bytes=64)
+        chunk_tiles = {}
+
+        def load_chunk(i):
+            cols = slice(i * CE, (i + 1) * CE)
+            g_t = loads.tile([P, CE], BF16, name="g_t")
+            load_by_batch(nc, g_t, g_flat[:, cols])
+            if i == 0:
+                load_by_batch(nc, v2, nq2)
+            u_t = loads.tile([P, CE], F32, name="u_t")
+            load_by_batch(nc, u_t, np2_flat[:, cols])
+            hd_t = loads.tile([P, CE], F32, name="hd_t")
+            load_by_batch(nc, hd_t, dot_flat[:, cols])
+            chunk_tiles[i] = {"g": g_t, "u": u_t, "hd": hd_t}
+
+        def roots(i):
+            tiles = chunk_tiles[i]
+            nc.scalar.activation(out=tiles["u"][:], in_=tiles["u"][:], func=ACT.Abs_reciprocal_sqrt)
+            w4_t = work.tile([P, CE], F32, name="w4_t")
+            nc.scalar.activation(out=w4_t[:], in_=tiles["u"][:], func=ACT.Square, scale=0.5)
+            tiles["w4"] = w4_t
+
+        def gradients(i):
+            tiles = chunk_tiles[i]
+            g_t, u_t, hd_t, w4_t = tiles["g"], tiles["u"], tiles["hd"], tiles["w4"]
+            a_t = work.tile([P, CE], F32, name="a_t")
+            ab_t = work.tile([P, 2, HALVES, KC, PACK], BF16, name="ab_t", align_bytes=64)
+            hs_t = work.tile([P, KC], F32, name="hs_t")
+            gq_t = work.tile([P, KC], F32, name="gq_t")
+            a_codes = work.tile([P, 2, HALVES, KC], U32, name="a_codes", align_bytes=64)
+            a_scales = work.tile([P, 2, HALVES, KC], U8, name="a_scales", align_bytes=64)
+            parts = [slice(t * TE, (t + 1) * TE) for t in range(TILES)]
+            rows = [slice(t * KT, (t + 1) * KT) for t in range(TILES)]
+            for t in range(TILES):
+                nc.vector.tensor_tensor(
+                    out=a_t[:, parts[t]].rearrange("b (k s) -> b k s", s=S),
+                    in0=g_t[:, parts[t]].rearrange("b (k s) -> b k s", s=S),
+                    in1=v2[:, i * KC + t * KT : i * KC + (t + 1) * KT].unsqueeze(2).to_broadcast([P, KT, S]),
+                    op=ALU.mult,
+                )
+            for t in range(TILES):
+                nc.vector.tensor_tensor(out=a_t[:, parts[t]], in0=a_t[:, parts[t]], in1=u_t[:, parts[t]], op=ALU.mult)
+            nc.scalar.activation(
+                out=ab_t[:, 0].rearrange("b h k j -> b k h j"),
+                in_=a_t[:].rearrange("b (k h j) -> b k h j", h=HALVES, j=PACK),
+                func=ACT.Copy,
+                scale=-0.5,
+            )
+            for t in range(TILES):
+                nc.vector.tensor_tensor(out=hd_t[:, parts[t]], in0=a_t[:, parts[t]], in1=hd_t[:, parts[t]], op=ALU.mult)
+            for t in range(TILES):
+                nc.vector.tensor_reduce(
+                    out=hs_t[:, rows[t]],
+                    in_=hd_t[:, parts[t]].rearrange("b (k s) -> b k s", s=S),
+                    axis=mybir.AxisListType.X,
+                    op=ALU.add,
+                )
+            for t in range(TILES):
+                nc.vector.tensor_tensor(
+                    out=ab_t[:, 1, :, rows[t], :].rearrange("b h k j -> b k h j"),
+                    in0=hd_t[:, parts[t]].rearrange("b (k h j) -> b k h j", h=HALVES, j=PACK),
+                    in1=w4_t[:, parts[t]].rearrange("b (k h j) -> b k h j", h=HALVES, j=PACK),
+                    op=ALU.mult,
+                )
+            nc.vector.tensor_tensor(out=gq_t[:], in0=hs_t[:], in1=inq[:, i * KC : (i + 1) * KC], op=ALU.mult)
+            nc.vector.quantize_mx(
+                out=a_codes[:].rearrange("b o h k -> b (o h k)").bitcast(E5M2X4),
+                scales=a_scales[:].rearrange("b o h k -> b (o h k)"),
+                in_=ab_t[:].rearrange("b o h k j -> b (o h k j)"),
+            )
+            tiles["gq"], tiles["codes"], tiles["scales"] = gq_t, a_codes, a_scales
+
+        def products(i):
+            tiles = chunk_tiles[i]
+            tiles["third"], tiles["mx"] = {}, {}
+            for t in range(TILES):
+                kt = slice(t * KT, (t + 1) * KT)
+                for dh in range(BANKS):
+                    dc = slice(dh * DT, (dh + 1) * DT)
+                    third_ps = psum_third.tile([KT, DT], F32, name="third_ps")
+                    nc.tensor.matmul(out=third_ps[:], lhsT=tiles["gq"][:, kt], rhs=ql2[:, dc], start=True, stop=True)
+                    mx_ps = psum_mx.tile([KT, DT], F32, name="mx_ps")
+                    for o in range(2):
+                        for h in range(HALVES):
+                            nc.tensor.matmul_mx(
+                                out=mx_ps[:],
+                                lhsT=tiles["codes"][:, o, h, kt].bitcast(E5M2X4),
+                                lhsT_scale=tiles["scales"][:, o, h, kt],
+                                rhs=x_codes[:, o, h, dc].bitcast(E4M3X4),
+                                rhs_scale=x_scales[:, o, h, dc],
+                                start=(o == 0 and h == 0),
+                                stop=(o == 1 and h == HALVES - 1),
+                            )
+                    tiles["third"][(t, dh)], tiles["mx"][(t, dh)] = third_ps, mx_ps
+
+        def finish(i, tail):
+            tiles = chunk_tiles[i]
+            outs = []
+            for t in range(TILES):
+                out_t = tail.tile([P, D], F32, name="out_t")
+                outs.append(out_t)
+                for dh in range(BANKS):
+                    dc = slice(dh * DT, (dh + 1) * DT)
+                    third_sb = tail.tile([KT, DT], F32, name="third_sb")
+                    nc.scalar.activation(out=third_sb[:], in_=tiles["third"][(t, dh)][:], func=ACT.Copy, scale=2.0)
+                    nc.vector.scalar_tensor_tensor(
+                        out=out_t[:, dc], in0=tiles["mx"][(t, dh)][:], scalar=2.0, in1=third_sb[:],
+                        op0=ALU.mult, op1=ALU.add,
+                    )
+            for t in range(TILES):
+                nc.vector.tensor_tensor(out=outs[t][:], in0=outs[t][:], in1=tiles["w"][:, t, :], op=ALU.mult)
+                row0 = i * KC + t * KT
+                nc.sync.dma_start(out=out[row0 : row0 + KT, :], in_=outs[t][:])
+
+        def load_w(i):
+            w_t = work.tile([P, TILES, D], BF16, name="w_t")
+            nc.sync.dma_start(out=w_t[:], in_=w_tiles[:, i * TILES : (i + 1) * TILES, :])
+            chunk_tiles[i]["w"] = w_t
+
+        load_chunk(0)
+        load_by_batch(nc, ql, q[:, S - 1, :])
+        with tc.tile_pool(name="xonce", bufs=1) as xonce, tc.tile_pool(name="xwork", bufs=2) as xwork:
+            p_t = xonce.tile([P, S, D], BF16)
+            load_by_batch(nc, p_t[:].rearrange("b s d -> b (s d)"), p_flat)
+            load_chunk(1)
+            load_chunk(2)
+            load_w(0)
+            nc.scalar.activation(out=v2[:], in_=v2[:], func=ACT.Abs_reciprocal_sqrt, scale=float(2 ** 18))
+            roots(0)
+            nc.scalar.activation(out=inq[:], in_=v2[:], func=ACT.Square, scale=256.0)
+            gradients(0)
+            grouped = {}
+            for h in range(HALVES):
+                rows = p_t[:, PACK * h : PACK * (h + 1), :]
+                x1g = xwork.tile([P, D, PACK], BF16, name="x1g", align_bytes=64)
+                nc.vector.tensor_tensor(
+                    out=x1g[:],
+                    in0=rows.rearrange("b j d -> b d j"),
+                    in1=ql[:].unsqueeze(2).to_broadcast([P, D, PACK]),
+                    op=ALU.mult,
+                )
+                x2g = xwork.tile([P, D, PACK], BF16, name="x2g", align_bytes=64)
+                nc.scalar.activation(
+                    out=x2g[:].rearrange("b (c i) j -> b c j i", i=4),
+                    in_=rows.rearrange("b j (c i) -> b c j i", i=4),
+                    func=ACT.Square,
+                )
+                grouped[h] = (x1g, x2g)
+            nc.scalar.activation(out=ql2[:], in_=ql[:], func=ACT.Square)
+            roots(1)
+            for o in range(2):
+                for h in range(HALVES):
+                    nc.vector.quantize_mx(
+                        out=x_codes[:, o, h, :].bitcast(E4M3X4),
+                        scales=x_scales[:, o, h, :],
+                        in_=grouped[h][o][:].rearrange("b d j -> b (d j)"),
+                    )
+
+        tail = ctx.enter_context(tc.tile_pool(name="tail", bufs=4))
+        for i in range(1, CHUNKS + 1):
+            if i + 2 < CHUNKS:
+                load_chunk(i + 2)
+            if i < CHUNKS:
+                load_w(i)
+            products(i - 1)
+            if i < CHUNKS:
+                gradients(i)
+            if i + 1 < CHUNKS:
+                roots(i + 1)
+            finish(i - 1, tail)

@@ -48,6 +48,9 @@ def tile_mpl_v_kernel(tc, p, q, W, dot, np2, nq2, grad_out, out):
     dot_flat = dot.rearrange("b k s -> b (k s)")
     np2_flat = np2.rearrange("b k s -> b (k s)")
     w_tiles = W.rearrange("(t r) d -> r t d", r=KT)
+    parts = [slice(t * TE, (t + 1) * TE) for t in range(TILES)]
+    rows = [slice(t * KT, (t + 1) * KT) for t in range(TILES)]
+    banks = [slice(c * DT, (c + 1) * DT) for c in range(BANKS)]
 
     with ExitStack() as ctx:
         ctx.enter_context(tc.manual_schedule())
@@ -57,8 +60,6 @@ def tile_mpl_v_kernel(tc, p, q, W, dot, np2, nq2, grad_out, out):
         psum_mx = ctx.enter_context(tc.psum_pool(name="psum_mx", bufs=4))
         psum_third = ctx.enter_context(tc.psum_pool(name="psum_third", bufs=4))
 
-        v2 = keep.tile([P, K], F32)
-        inq = keep.tile([P, K], F32)
         ql = keep.tile([P, D], BF16)
         ql2 = keep.tile([P, D], F32)
         x_codes = keep.tile([P, 2, HALVES, D], U32, align_bytes=64)
@@ -67,39 +68,44 @@ def tile_mpl_v_kernel(tc, p, q, W, dot, np2, nq2, grad_out, out):
 
         def load_chunk(i):
             cols = slice(i * CE, (i + 1) * CE)
-            g_t = loads.tile([P, CE], BF16, name="g_t")
-            load_by_batch(nc, g_t, g_flat[:, cols])
-            if i == 0:
-                load_by_batch(nc, v2, nq2)
             u_t = loads.tile([P, CE], F32, name="u_t")
             load_by_batch(nc, u_t, np2_flat[:, cols])
+            v2_t = loads.tile([P, KC], F32, name="v2_t")
+            load_by_batch(nc, v2_t, nq2[:, i * KC : (i + 1) * KC])
+            g_t = loads.tile([P, CE], BF16, name="g_t")
+            load_by_batch(nc, g_t, g_flat[:, cols])
             hd_t = loads.tile([P, CE], F32, name="hd_t")
             load_by_batch(nc, hd_t, dot_flat[:, cols])
-            chunk_tiles[i] = {"g": g_t, "u": u_t, "hd": hd_t}
+            chunk_tiles[i] = {"g": g_t, "u": u_t, "hd": hd_t, "v2": v2_t}
+
+        def load_w(i):
+            w_t = loads.tile([P, TILES, D], BF16, name="w_t")
+            nc.sync.dma_start(out=w_t[:], in_=w_tiles[:, i * TILES : (i + 1) * TILES, :])
+            chunk_tiles[i]["w"] = w_t
 
         def roots(i):
             tiles = chunk_tiles[i]
-            nc.scalar.activation(out=tiles["u"][:], in_=tiles["u"][:], func=ACT.Abs_reciprocal_sqrt)
             w4_t = work.tile([P, CE], F32, name="w4_t")
+            inq_t = work.tile([P, KC], F32, name="inq_t")
+            nc.scalar.activation(out=tiles["u"][:], in_=tiles["u"][:], func=ACT.Abs_reciprocal_sqrt)
+            nc.scalar.activation(
+                out=tiles["v2"][:], in_=tiles["v2"][:], func=ACT.Abs_reciprocal_sqrt, scale=float(2 ** 18)
+            )
             nc.scalar.activation(out=w4_t[:], in_=tiles["u"][:], func=ACT.Square, scale=0.5)
-            tiles["w4"] = w4_t
+            nc.scalar.activation(out=inq_t[:], in_=tiles["v2"][:], func=ACT.Square, scale=256.0)
+            tiles["w4"], tiles["inq"] = w4_t, inq_t
 
-        def gradients(i):
+        def gradients_first(i):
             tiles = chunk_tiles[i]
-            g_t, u_t, hd_t, w4_t = tiles["g"], tiles["u"], tiles["hd"], tiles["w4"]
+            g_t, u_t, hd_t = tiles["g"], tiles["u"], tiles["hd"]
             a_t = work.tile([P, CE], F32, name="a_t")
             ab_t = work.tile([P, 2, HALVES, KC, PACK], BF16, name="ab_t", align_bytes=64)
             hs_t = work.tile([P, KC], F32, name="hs_t")
-            gq_t = work.tile([P, KC], F32, name="gq_t")
-            a_codes = work.tile([P, 2, HALVES, KC], U32, name="a_codes", align_bytes=64)
-            a_scales = work.tile([P, 2, HALVES, KC], U8, name="a_scales", align_bytes=64)
-            parts = [slice(t * TE, (t + 1) * TE) for t in range(TILES)]
-            rows = [slice(t * KT, (t + 1) * KT) for t in range(TILES)]
             for t in range(TILES):
                 nc.vector.tensor_tensor(
                     out=a_t[:, parts[t]].rearrange("b (k s) -> b k s", s=S),
                     in0=g_t[:, parts[t]].rearrange("b (k s) -> b k s", s=S),
-                    in1=v2[:, i * KC + t * KT : i * KC + (t + 1) * KT].unsqueeze(2).to_broadcast([P, KT, S]),
+                    in1=tiles["v2"][:, rows[t]].unsqueeze(2).to_broadcast([P, KT, S]),
                     op=ALU.mult,
                 )
             for t in range(TILES):
@@ -119,18 +125,25 @@ def tile_mpl_v_kernel(tc, p, q, W, dot, np2, nq2, grad_out, out):
                     axis=mybir.AxisListType.X,
                     op=ALU.add,
                 )
+            tiles["ab"], tiles["hs"] = ab_t, hs_t
+
+        def gradients_second(i):
+            tiles = chunk_tiles[i]
+            gq_t = work.tile([P, KC], F32, name="gq_t")
+            a_codes = work.tile([P, 2, HALVES, KC], U32, name="a_codes", align_bytes=64)
+            a_scales = work.tile([P, 2, HALVES, KC], U8, name="a_scales", align_bytes=64)
             for t in range(TILES):
                 nc.vector.tensor_tensor(
-                    out=ab_t[:, 1, :, rows[t], :].rearrange("b h k j -> b k h j"),
-                    in0=hd_t[:, parts[t]].rearrange("b (k h j) -> b k h j", h=HALVES, j=PACK),
-                    in1=w4_t[:, parts[t]].rearrange("b (k h j) -> b k h j", h=HALVES, j=PACK),
+                    out=tiles["ab"][:, 1, :, rows[t], :].rearrange("b h k j -> b k h j"),
+                    in0=tiles["hd"][:, parts[t]].rearrange("b (k h j) -> b k h j", h=HALVES, j=PACK),
+                    in1=tiles["w4"][:, parts[t]].rearrange("b (k h j) -> b k h j", h=HALVES, j=PACK),
                     op=ALU.mult,
                 )
-            nc.vector.tensor_tensor(out=gq_t[:], in0=hs_t[:], in1=inq[:, i * KC : (i + 1) * KC], op=ALU.mult)
+            nc.vector.tensor_tensor(out=gq_t[:], in0=tiles["hs"][:], in1=tiles["inq"][:], op=ALU.mult)
             nc.vector.quantize_mx(
                 out=a_codes[:].rearrange("b o h k -> b (o h k)").bitcast(E5M2X4),
                 scales=a_scales[:].rearrange("b o h k -> b (o h k)"),
-                in_=ab_t[:].rearrange("b o h k j -> b (o h k j)"),
+                in_=tiles["ab"][:].rearrange("b o h k j -> b (o h k j)"),
             )
             tiles["gq"], tiles["codes"], tiles["scales"] = gq_t, a_codes, a_scales
 
@@ -138,48 +151,49 @@ def tile_mpl_v_kernel(tc, p, q, W, dot, np2, nq2, grad_out, out):
             tiles = chunk_tiles[i]
             tiles["third"], tiles["mx"] = {}, {}
             for t in range(TILES):
-                kt = slice(t * KT, (t + 1) * KT)
-                for dh in range(BANKS):
-                    dc = slice(dh * DT, (dh + 1) * DT)
+                for c in range(BANKS):
                     third_ps = psum_third.tile([KT, DT], F32, name="third_ps")
-                    nc.tensor.matmul(out=third_ps[:], lhsT=tiles["gq"][:, kt], rhs=ql2[:, dc], start=True, stop=True)
+                    nc.tensor.matmul(
+                        out=third_ps[:], lhsT=tiles["gq"][:, rows[t]], rhs=ql2[:, banks[c]], start=True, stop=True
+                    )
                     mx_ps = psum_mx.tile([KT, DT], F32, name="mx_ps")
                     for o in range(2):
                         for h in range(HALVES):
                             nc.tensor.matmul_mx(
                                 out=mx_ps[:],
-                                lhsT=tiles["codes"][:, o, h, kt].bitcast(E5M2X4),
-                                lhsT_scale=tiles["scales"][:, o, h, kt],
-                                rhs=x_codes[:, o, h, dc].bitcast(E4M3X4),
-                                rhs_scale=x_scales[:, o, h, dc],
+                                lhsT=tiles["codes"][:, o, h, rows[t]].bitcast(E5M2X4),
+                                lhsT_scale=tiles["scales"][:, o, h, rows[t]],
+                                rhs=x_codes[:, o, h, banks[c]].bitcast(E4M3X4),
+                                rhs_scale=x_scales[:, o, h, banks[c]],
                                 start=(o == 0 and h == 0),
                                 stop=(o == 1 and h == HALVES - 1),
                             )
-                    tiles["third"][(t, dh)], tiles["mx"][(t, dh)] = third_ps, mx_ps
+                    tiles["third"][(t, c)], tiles["mx"][(t, c)] = third_ps, mx_ps
 
-        def finish(i, tail):
+        def add_terms(i, tail):
             tiles = chunk_tiles[i]
-            outs = []
+            tiles["out"] = []
             for t in range(TILES):
                 out_t = tail.tile([P, D], F32, name="out_t")
-                outs.append(out_t)
-                for dh in range(BANKS):
-                    dc = slice(dh * DT, (dh + 1) * DT)
+                tiles["out"].append(out_t)
+                for c in range(BANKS):
                     third_sb = tail.tile([KT, DT], F32, name="third_sb")
-                    nc.scalar.activation(out=third_sb[:], in_=tiles["third"][(t, dh)][:], func=ACT.Copy, scale=2.0)
+                    nc.scalar.activation(out=third_sb[:], in_=tiles["third"][(t, c)][:], func=ACT.Copy, scale=2.0)
                     nc.vector.scalar_tensor_tensor(
-                        out=out_t[:, dc], in0=tiles["mx"][(t, dh)][:], scalar=2.0, in1=third_sb[:],
+                        out=out_t[:, banks[c]], in0=tiles["mx"][(t, c)][:], scalar=2.0, in1=third_sb[:],
                         op0=ALU.mult, op1=ALU.add,
                     )
-            for t in range(TILES):
-                nc.vector.tensor_tensor(out=outs[t][:], in0=outs[t][:], in1=tiles["w"][:, t, :], op=ALU.mult)
-                row0 = i * KC + t * KT
-                nc.sync.dma_start(out=out[row0 : row0 + KT, :], in_=outs[t][:])
 
-        def load_w(i):
-            w_t = work.tile([P, TILES, D], BF16, name="w_t")
-            nc.sync.dma_start(out=w_t[:], in_=w_tiles[:, i * TILES : (i + 1) * TILES, :])
-            chunk_tiles[i]["w"] = w_t
+        def scale_and_store(i):
+            tiles = chunk_tiles[i]
+            for t in range(TILES):
+                out_t = tiles["out"][t]
+                for c in range(BANKS):
+                    nc.vector.tensor_tensor(
+                        out=out_t[:, banks[c]], in0=out_t[:, banks[c]], in1=tiles["w"][:, t, banks[c]], op=ALU.mult
+                    )
+                row0 = i * KC + t * KT
+                nc.sync.dma_start(out=out[row0 : row0 + KT, :], in_=out_t[:])
 
         load_chunk(0)
         load_by_batch(nc, ql, q[:, S - 1, :])
@@ -189,24 +203,23 @@ def tile_mpl_v_kernel(tc, p, q, W, dot, np2, nq2, grad_out, out):
             load_chunk(1)
             load_chunk(2)
             load_w(0)
-            nc.scalar.activation(out=v2[:], in_=v2[:], func=ACT.Abs_reciprocal_sqrt, scale=float(2 ** 18))
             roots(0)
-            nc.scalar.activation(out=inq[:], in_=v2[:], func=ACT.Square, scale=256.0)
-            gradients(0)
+            gradients_first(0)
+            gradients_second(0)
             grouped = {}
             for h in range(HALVES):
-                rows = p_t[:, PACK * h : PACK * (h + 1), :]
+                p_rows = p_t[:, PACK * h : PACK * (h + 1), :]
                 x1g = xwork.tile([P, D, PACK], BF16, name="x1g", align_bytes=64)
                 nc.vector.tensor_tensor(
                     out=x1g[:],
-                    in0=rows.rearrange("b j d -> b d j"),
+                    in0=p_rows.rearrange("b j d -> b d j"),
                     in1=ql[:].unsqueeze(2).to_broadcast([P, D, PACK]),
                     op=ALU.mult,
                 )
                 x2g = xwork.tile([P, D, PACK], BF16, name="x2g", align_bytes=64)
                 nc.scalar.activation(
                     out=x2g[:].rearrange("b (c i) j -> b c j i", i=4),
-                    in_=rows.rearrange("b j (c i) -> b c j i", i=4),
+                    in_=p_rows.rearrange("b j (c i) -> b c j i", i=4),
                     func=ACT.Square,
                 )
                 grouped[h] = (x1g, x2g)
@@ -228,7 +241,10 @@ def tile_mpl_v_kernel(tc, p, q, W, dot, np2, nq2, grad_out, out):
                 load_w(i)
             products(i - 1)
             if i < CHUNKS:
-                gradients(i)
+                gradients_first(i)
+            add_terms(i - 1, tail)
+            if i < CHUNKS:
+                gradients_second(i)
             if i + 1 < CHUNKS:
                 roots(i + 1)
-            finish(i - 1, tail)
+            scale_and_store(i - 1)

@@ -189,7 +189,7 @@ def tile_mpl_v_kernel(tc, p, q, W, dot, np2, nq2, grad_out, out):
             for t in range(TILES):
                 out_t = tiles["out"][t]
                 for c in range(BANKS):
-                    nc.vector.tensor_tensor(
+                    nc.gpsimd.tensor_tensor(
                         out=out_t[:, banks[c]], in0=out_t[:, banks[c]], in1=tiles["w"][:, t, banks[c]], op=ALU.mult
                     )
                 row0 = i * KC + t * KT

@@ -1,6 +1,7 @@
 from contextlib import ExitStack
 
 import concourse.mybir as mybir
+from concourse.masks import make_identity
 
 F32 = mybir.dt.float32
 BF16 = mybir.dt.bfloat16
@@ -18,11 +19,11 @@ K = 2048
 PACK = 4
 HALVES = S // PACK
 KT = 128
-TILES = 2
+WIDTHS = (2, 2, 2, 2, 2, 2, 2, 1, 1)
+CHUNKS = len(WIDTHS)
+TILES = max(WIDTHS)
 KC = KT * TILES
-CHUNKS = K // KC
 CE = KC * S
-TE = KT * S
 DT = 512
 BANKS = D // DT
 
@@ -43,169 +44,259 @@ def load_by_batch(nc, dst, src):
 
 def tile_mpl_v_kernel(tc, p, q, W, dot, np2, nq2, grad_out, out):
     nc = tc.nc
-    p_flat = p.rearrange("b s d -> b (s d)")
     g_flat = grad_out.rearrange("b s k -> b (s k)")
     dot_flat = dot.rearrange("b k s -> b (k s)")
     np2_flat = np2.rearrange("b k s -> b (k s)")
     w_tiles = W.rearrange("(t r) d -> r t d", r=KT)
-    parts = [slice(t * TE, (t + 1) * TE) for t in range(TILES)]
     rows = [slice(t * KT, (t + 1) * KT) for t in range(TILES)]
     banks = [slice(c * DT, (c + 1) * DT) for c in range(BANKS)]
+    tile0 = [sum(WIDTHS[:i]) for i in range(CHUNKS)]
+    kc = [KT * n for n in WIDTHS]
+    ce = [KT * n * S for n in WIDTHS]
+    ks = [slice(KT * tile0[i], KT * tile0[i] + kc[i]) for i in range(CHUNKS)]
+    es = [slice(KT * tile0[i] * S, KT * tile0[i] * S + ce[i]) for i in range(CHUNKS)]
+
+    def live(i):
+        return 0 <= i < CHUNKS
+
+    def units(i):
+        return [(t, c) for t in range(WIDTHS[i]) for c in range(BANKS)]
 
     with ExitStack() as ctx:
         ctx.enter_context(tc.manual_schedule())
         keep = ctx.enter_context(tc.tile_pool(name="keep", bufs=1))
-        loads = ctx.enter_context(tc.tile_pool(name="loads", bufs=3))
-        work = ctx.enter_context(tc.tile_pool(name="work", bufs=2))
+        three = ctx.enter_context(tc.tile_pool(name="three", bufs=3))
+        two = ctx.enter_context(tc.tile_pool(name="two", bufs=2))
         psum_mx = ctx.enter_context(tc.psum_pool(name="psum_mx", bufs=4))
-        psum_third = ctx.enter_context(tc.psum_pool(name="psum_third", bufs=4))
+        psum_third = ctx.enter_context(tc.psum_pool(name="psum_third", bufs=3))
+        psum_sums = ctx.enter_context(tc.psum_pool(name="psum_sums", bufs=1))
 
+        ident = keep.tile([P, P], F32)
+        make_identity(nc, ident[:])
         ql = keep.tile([P, D], BF16)
         ql2 = keep.tile([P, D], F32)
+        v2_all = keep.tile([P, K], F32)
+        inq_all = keep.tile([P, K], F32)
         x_codes = keep.tile([P, 2, HALVES, D], U32, align_bytes=64)
         x_scales = keep.tile([P, 2, HALVES, D], U8, align_bytes=64)
-        chunk_tiles = {}
+        st = [{} for i in range(CHUNKS)]
+        late = {}
 
-        def load_chunk(i):
-            cols = slice(i * CE, (i + 1) * CE)
-            u_t = loads.tile([P, CE], F32, name="u_t")
-            load_by_batch(nc, u_t, np2_flat[:, cols])
-            v2_t = loads.tile([P, KC], F32, name="v2_t")
-            load_by_batch(nc, v2_t, nq2[:, i * KC : (i + 1) * KC])
-            g_t = loads.tile([P, CE], BF16, name="g_t")
-            load_by_batch(nc, g_t, g_flat[:, cols])
-            hd_t = loads.tile([P, CE], F32, name="hd_t")
-            load_by_batch(nc, hd_t, dot_flat[:, cols])
-            chunk_tiles[i] = {"g": g_t, "u": u_t, "hd": hd_t, "v2": v2_t}
+        def grouped_view(ap):
+            return ap.rearrange("b (h k j) -> b k h j", h=HALVES, j=PACK)
+
+        def natural_view(ap):
+            return ap.rearrange("b (k h j) -> b k h j", h=HALVES, j=PACK)
+
+        def load_np2(i):
+            u_t = three.tile([P, CE], F32, name="u_t")
+            load_by_batch(nc, u_t[:, : ce[i]], np2_flat[:, es[i]])
+            st[i]["u"] = u_t[:, : ce[i]]
+
+        def load_g(i):
+            g_t = three.tile([P, CE], BF16, name="g_t")
+            load_by_batch(nc, g_t[:, : ce[i]], g_flat[:, es[i]])
+            st[i]["g"] = g_t[:, : ce[i]]
+
+        def load_dot(i):
+            hd_t = three.tile([P, CE], F32, name="hd_t")
+            load_by_batch(nc, hd_t[:, : ce[i]], dot_flat[:, es[i]])
+            st[i]["hd"] = hd_t[:, : ce[i]]
 
         def load_w(i):
-            w_t = loads.tile([P, TILES, D], BF16, name="w_t")
-            nc.sync.dma_start(out=w_t[:], in_=w_tiles[:, i * TILES : (i + 1) * TILES, :])
-            chunk_tiles[i]["w"] = w_t
+            w_t = late["two"].tile([P, TILES, D], BF16, name="w_t")
+            nc.sync.dma_start(out=w_t[:, : WIDTHS[i], :], in_=w_tiles[:, tile0[i] : tile0[i] + WIDTHS[i], :])
+            st[i]["w"] = w_t
 
-        def roots(i):
-            tiles = chunk_tiles[i]
-            w4_t = work.tile([P, CE], F32, name="w4_t")
-            inq_t = work.tile([P, KC], F32, name="inq_t")
-            nc.scalar.activation(out=tiles["u"][:], in_=tiles["u"][:], func=ACT.Abs_reciprocal_sqrt)
+        def roots_q(cols):
             nc.scalar.activation(
-                out=tiles["v2"][:], in_=tiles["v2"][:], func=ACT.Abs_reciprocal_sqrt, scale=float(2 ** 18)
+                out=v2_all[:, cols], in_=v2_all[:, cols], func=ACT.Abs_reciprocal_sqrt, scale=float(2 ** 18)
             )
-            nc.scalar.activation(out=w4_t[:], in_=tiles["u"][:], func=ACT.Square, scale=0.5)
-            nc.scalar.activation(out=inq_t[:], in_=tiles["v2"][:], func=ACT.Square, scale=256.0)
-            tiles["w4"], tiles["inq"] = w4_t, inq_t
+            nc.scalar.activation(out=inq_all[:, cols], in_=v2_all[:, cols], func=ACT.Square, scale=256.0)
 
-        def gradients_first(i):
-            tiles = chunk_tiles[i]
-            g_t, u_t, hd_t = tiles["g"], tiles["u"], tiles["hd"]
-            a_t = work.tile([P, CE], F32, name="a_t")
-            ab_t = work.tile([P, 2, HALVES, KC, PACK], BF16, name="ab_t", align_bytes=64)
-            hs_t = work.tile([P, KC], F32, name="hs_t")
-            for t in range(TILES):
-                nc.vector.tensor_tensor(
-                    out=a_t[:, parts[t]].rearrange("b (k s) -> b k s", s=S),
-                    in0=g_t[:, parts[t]].rearrange("b (k s) -> b k s", s=S),
-                    in1=tiles["v2"][:, rows[t]].unsqueeze(2).to_broadcast([P, KT, S]),
-                    op=ALU.mult,
-                )
-            for t in range(TILES):
-                nc.vector.tensor_tensor(out=a_t[:, parts[t]], in0=a_t[:, parts[t]], in1=u_t[:, parts[t]], op=ALU.mult)
+        def root_u(i):
+            nc.scalar.activation(out=st[i]["u"], in_=st[i]["u"], func=ACT.Abs_reciprocal_sqrt)
+
+        def square_u(i):
+            w4_t = two.tile([P, CE], F32, name="w4_t")
+            nc.scalar.activation(out=w4_t[:, : ce[i]], in_=st[i]["u"], func=ACT.Square, scale=0.5)
+            st[i]["w4"] = w4_t[:, : ce[i]]
+
+        def round_g_dot(i):
+            ab_t = two.tile([P, 2, CE], BF16, name="ab_t", align_bytes=64)
             nc.scalar.activation(
-                out=ab_t[:, 0].rearrange("b h k j -> b k h j"),
-                in_=a_t[:].rearrange("b (k h j) -> b k h j", h=HALVES, j=PACK),
-                func=ACT.Copy,
-                scale=-0.5,
+                out=grouped_view(ab_t[:, 0, : ce[i]]), in_=natural_view(st[i]["a"]), func=ACT.Copy, scale=-0.5
             )
-            for t in range(TILES):
-                nc.vector.tensor_tensor(out=hd_t[:, parts[t]], in0=a_t[:, parts[t]], in1=hd_t[:, parts[t]], op=ALU.mult)
-            for t in range(TILES):
-                nc.vector.tensor_reduce(
-                    out=hs_t[:, rows[t]],
-                    in_=hd_t[:, parts[t]].rearrange("b (k s) -> b k s", s=S),
-                    axis=mybir.AxisListType.X,
-                    op=ALU.add,
-                )
-            tiles["ab"], tiles["hs"] = ab_t, hs_t
+            st[i]["ab"] = ab_t
 
-        def gradients_second(i):
-            tiles = chunk_tiles[i]
-            gq_t = work.tile([P, KC], F32, name="gq_t")
-            a_codes = work.tile([P, 2, HALVES, KC], U32, name="a_codes", align_bytes=64)
-            a_scales = work.tile([P, 2, HALVES, KC], U8, name="a_scales", align_bytes=64)
-            for t in range(TILES):
-                nc.vector.tensor_tensor(
-                    out=tiles["ab"][:, 1, :, rows[t], :].rearrange("b h k j -> b k h j"),
-                    in0=tiles["hd"][:, parts[t]].rearrange("b (k h j) -> b k h j", h=HALVES, j=PACK),
-                    in1=tiles["w4"][:, parts[t]].rearrange("b (k h j) -> b k h j", h=HALVES, j=PACK),
-                    op=ALU.mult,
-                )
-            nc.vector.tensor_tensor(out=gq_t[:], in0=tiles["hs"][:], in1=tiles["inq"][:], op=ALU.mult)
-            nc.vector.quantize_mx(
-                out=a_codes[:].rearrange("b o h k -> b (o h k)").bitcast(E5M2X4),
-                scales=a_scales[:].rearrange("b o h k -> b (o h k)"),
-                in_=tiles["ab"][:].rearrange("b o h k j -> b (o h k j)"),
+        def copy_sums(i):
+            sums_sb = two.tile([P, KC], F32, name="sums_sb")
+            nc.scalar.copy(out=sums_sb[:, : kc[i]], in_=st[i]["sums"][:, : kc[i]])
+            st[i]["sums_sb"] = sums_sb
+
+        def times_v(i):
+            a_t = two.tile([P, CE], F32, name="a_t")
+            nc.vector.tensor_tensor(
+                out=a_t[:, : ce[i]].rearrange("b (k s) -> b k s", s=S),
+                in0=st[i]["g"].rearrange("b (k s) -> b k s", s=S),
+                in1=v2_all[:, ks[i]].unsqueeze(2).to_broadcast([P, kc[i], S]),
+                op=ALU.mult,
             )
-            tiles["gq"], tiles["codes"], tiles["scales"] = gq_t, a_codes, a_scales
+            st[i]["a"] = a_t[:, : ce[i]]
 
-        def products(i):
-            tiles = chunk_tiles[i]
-            tiles["third"], tiles["mx"] = {}, {}
-            for t in range(TILES):
-                for c in range(BANKS):
-                    third_ps = psum_third.tile([KT, DT], F32, name="third_ps")
-                    nc.tensor.matmul(
-                        out=third_ps[:], lhsT=tiles["gq"][:, rows[t]], rhs=ql2[:, banks[c]], start=True, stop=True
-                    )
-                    mx_ps = psum_mx.tile([KT, DT], F32, name="mx_ps")
-                    for o in range(2):
-                        for h in range(HALVES):
-                            nc.tensor.matmul_mx(
-                                out=mx_ps[:],
-                                lhsT=tiles["codes"][:, o, h, rows[t]].bitcast(E5M2X4),
-                                lhsT_scale=tiles["scales"][:, o, h, rows[t]],
-                                rhs=x_codes[:, o, h, banks[c]].bitcast(E4M3X4),
-                                rhs_scale=x_scales[:, o, h, banks[c]],
-                                start=(o == 0 and h == 0),
-                                stop=(o == 1 and h == HALVES - 1),
-                            )
-                    tiles["third"][(t, c)], tiles["mx"][(t, c)] = third_ps, mx_ps
+        def times_u(i):
+            nc.vector.tensor_tensor(out=st[i]["a"], in0=st[i]["a"], in1=st[i]["u"], op=ALU.mult)
 
-        def add_terms(i, tail):
-            tiles = chunk_tiles[i]
-            tiles["out"] = []
-            for t in range(TILES):
-                out_t = tail.tile([P, D], F32, name="out_t")
-                tiles["out"].append(out_t)
+        def times_dot(i):
+            nc.vector.tensor_tensor(out=st[i]["hd"], in0=st[i]["a"], in1=st[i]["hd"], op=ALU.mult)
+
+        def over_nq2(i):
+            gq_t = two.tile([P, KC], F32, name="gq_t")
+            nc.vector.tensor_tensor(
+                out=gq_t[:, : kc[i]], in0=st[i]["sums"][:, KC : KC + kc[i]], in1=inq_all[:, ks[i]], op=ALU.mult
+            )
+            st[i]["gq"] = gq_t
+
+        def over_np2(i):
+            nc.vector.tensor_tensor(
+                out=grouped_view(st[i]["ab"][:, 1, : ce[i]]),
+                in0=natural_view(st[i]["hd"]),
+                in1=natural_view(st[i]["w4"]),
+                op=ALU.mult,
+            )
+
+        def quantize(i):
+            a_codes = two.tile([P, 2, HALVES * KC], U32, name="a_codes", align_bytes=64)
+            a_scales = two.tile([P, 2, HALVES * KC], U8, name="a_scales", align_bytes=64)
+            for o in range(2):
+                nc.vector.quantize_mx(
+                    out=a_codes[:, o, : HALVES * kc[i]].bitcast(E5M2X4),
+                    scales=a_scales[:, o, : HALVES * kc[i]],
+                    in_=st[i]["ab"][:, o, : ce[i]],
+                )
+            st[i]["codes"], st[i]["scales"] = a_codes, a_scales
+
+        def add_terms(i):
+            st[i]["out"] = []
+            for t in range(WIDTHS[i]):
+                out_t = late["four"].tile([P, D], F32, name="out_t")
+                st[i]["out"].append(out_t)
                 for c in range(BANKS):
-                    third_sb = tail.tile([KT, DT], F32, name="third_sb")
-                    nc.scalar.activation(out=third_sb[:], in_=tiles["third"][(t, c)][:], func=ACT.Copy, scale=2.0)
                     nc.vector.scalar_tensor_tensor(
-                        out=out_t[:, banks[c]], in0=tiles["mx"][(t, c)][:], scalar=2.0, in1=third_sb[:],
+                        out=out_t[:, banks[c]], in0=st[i]["mx"][(t, c)][:], scalar=2.0, in1=st[i]["third"][(t, c)][:],
                         op0=ALU.mult, op1=ALU.add,
                     )
 
         def scale_and_store(i):
-            tiles = chunk_tiles[i]
-            for t in range(TILES):
-                out_t = tiles["out"][t]
+            for t in range(WIDTHS[i]):
+                out_t = st[i]["out"][t]
                 for c in range(BANKS):
                     nc.gpsimd.tensor_tensor(
-                        out=out_t[:, banks[c]], in0=out_t[:, banks[c]], in1=tiles["w"][:, t, banks[c]], op=ALU.mult
+                        out=out_t[:, banks[c]], in0=out_t[:, banks[c]], in1=st[i]["w"][:, t, banks[c]], op=ALU.mult
                     )
-                row0 = i * KC + t * KT
+                row0 = (tile0[i] + t) * KT
                 nc.sync.dma_start(out=out[row0 : row0 + KT, :], in_=out_t[:])
 
-        load_chunk(0)
+        def sum_over_s(i):
+            sums = psum_sums.tile([P, 2 * KC], F32, name="sums")
+            for t in range(WIDTHS[i]):
+                for s in range(S):
+                    nc.tensor.matmul(
+                        out=sums[:, rows[t]],
+                        lhsT=st[i]["hd"][:, t * KT * S + s : (t + 1) * KT * S : S],
+                        rhs=ident[:],
+                        is_transpose=True,
+                        start=(s == 0),
+                        stop=(s == S - 1),
+                    )
+            st[i]["sums"] = sums
+
+        def turn_back(i):
+            for t in range(WIDTHS[i]):
+                nc.tensor.transpose(st[i]["sums"][:, KC + t * KT : KC + (t + 1) * KT], st[i]["sums_sb"][:, rows[t]], ident[:])
+
+        def products_mx(i):
+            st[i]["mx"] = {}
+            for t, c in units(i):
+                mx_ps = psum_mx.tile([KT, DT], F32, name="mx_ps")
+                for o in range(2):
+                    for h in range(HALVES):
+                        cols = slice(h * kc[i] + t * KT, h * kc[i] + (t + 1) * KT)
+                        nc.tensor.matmul_mx(
+                            out=mx_ps[:],
+                            lhsT=st[i]["codes"][:, o, cols].bitcast(E5M2X4),
+                            lhsT_scale=st[i]["scales"][:, o, cols],
+                            rhs=x_codes[:, o, h, banks[c]].bitcast(E4M3X4),
+                            rhs_scale=x_scales[:, o, h, banks[c]],
+                            start=(o == 0 and h == 0),
+                            stop=(o == 1 and h == HALVES - 1),
+                        )
+                st[i]["mx"][(t, c)] = mx_ps
+
+        def products_third(i):
+            st[i]["third"] = {}
+            for t, c in units(i):
+                third_ps = psum_third.tile([KT, DT], F32, name="third_ps")
+                nc.tensor.matmul(
+                    out=third_ps[:], lhsT=st[i]["gq"][:, rows[t]], rhs=ql2[:, banks[c]], start=True, stop=True
+                )
+                third_sb = late["four"].tile([KT, DT], F32, name="third_sb")
+                nc.scalar.activation(out=third_sb[:], in_=third_ps[:], func=ACT.Copy, scale=2.0)
+                st[i]["third"][(t, c)] = third_sb
+
+        def period(j):
+            if live(j + 3):
+                load_np2(j + 3)
+                load_g(j + 3)
+            if live(j + 2):
+                load_dot(j + 2)
+            if live(j - 1):
+                load_w(j - 1)
+            if live(j + 2):
+                root_u(j + 2)
+            if live(j + 1):
+                square_u(j + 1)
+            if live(j - 1):
+                turn_back(j - 1)
+            if live(j - 2):
+                add_terms(j - 2)
+                scale_and_store(j - 2)
+            if live(j - 1):
+                products_mx(j - 1)
+                over_nq2(j - 1)
+                products_third(j - 1)
+            if live(j + 1):
+                times_v(j + 1)
+            if live(j):
+                times_dot(j)
+                sum_over_s(j)
+            if live(j + 1):
+                times_u(j + 1)
+                round_g_dot(j + 1)
+            if live(j):
+                over_np2(j)
+                quantize(j)
+                copy_sums(j)
+
         load_by_batch(nc, ql, q[:, S - 1, :])
         with tc.tile_pool(name="xonce", bufs=1) as xonce, tc.tile_pool(name="xwork", bufs=2) as xwork:
             p_t = xonce.tile([P, S, D], BF16)
-            load_by_batch(nc, p_t[:].rearrange("b s d -> b (s d)"), p_flat)
-            load_chunk(1)
-            load_chunk(2)
-            load_w(0)
-            roots(0)
-            gradients_first(0)
-            gradients_second(0)
+            for h in range(HALVES):
+                load_by_batch(
+                    nc,
+                    p_t[:, PACK * h : PACK * (h + 1), :].rearrange("b s d -> b (s d)"),
+                    p[:, PACK * h : PACK * (h + 1), :].rearrange("b s d -> b (s d)"),
+                )
+            load_by_batch(nc, v2_all[:, : 2 * KC], nq2[:, : 2 * KC])
+            load_g(0)
+            load_np2(0)
+            load_dot(0)
+            load_g(1)
+            load_np2(1)
+            load_by_batch(nc, v2_all[:, 2 * KC :], nq2[:, 2 * KC :])
+            load_dot(1)
+            load_g(2)
+            load_np2(2)
             grouped = {}
             for h in range(HALVES):
                 p_rows = p_t[:, PACK * h : PACK * (h + 1), :]
@@ -223,28 +314,30 @@ def tile_mpl_v_kernel(tc, p, q, W, dot, np2, nq2, grad_out, out):
                     func=ACT.Square,
                 )
                 grouped[h] = (x1g, x2g)
+                if h == 0:
+                    roots_q(slice(0, 2 * KC))
+                    root_u(0)
+            times_v(0)
+            for h in range(HALVES):
+                nc.vector.quantize_mx(
+                    out=x_codes[:, 0, h, :].bitcast(E4M3X4),
+                    scales=x_scales[:, 0, h, :],
+                    in_=grouped[h][0][:].rearrange("b d j -> b (d j)"),
+                )
+            times_u(0)
+            round_g_dot(0)
+            for h in range(HALVES):
+                nc.vector.quantize_mx(
+                    out=x_codes[:, 1, h, :].bitcast(E4M3X4),
+                    scales=x_scales[:, 1, h, :],
+                    in_=grouped[h][1][:].rearrange("b d j -> b (d j)"),
+                )
+            square_u(0)
+            root_u(1)
             nc.scalar.activation(out=ql2[:], in_=ql[:], func=ACT.Square)
-            roots(1)
-            for o in range(2):
-                for h in range(HALVES):
-                    nc.vector.quantize_mx(
-                        out=x_codes[:, o, h, :].bitcast(E4M3X4),
-                        scales=x_scales[:, o, h, :],
-                        in_=grouped[h][o][:].rearrange("b d j -> b (d j)"),
-                    )
+            roots_q(slice(2 * KC, K))
 
-        tail = ctx.enter_context(tc.tile_pool(name="tail", bufs=4))
-        for i in range(1, CHUNKS + 1):
-            if i + 2 < CHUNKS:
-                load_chunk(i + 2)
-            if i < CHUNKS:
-                load_w(i)
-            products(i - 1)
-            if i < CHUNKS:
-                gradients_first(i)
-            add_terms(i - 1, tail)
-            if i < CHUNKS:
-                gradients_second(i)
-            if i + 1 < CHUNKS:
-                roots(i + 1)
-            scale_and_store(i - 1)
+        late["two"] = ctx.enter_context(tc.tile_pool(name="late_two", bufs=2))
+        late["four"] = ctx.enter_context(tc.tile_pool(name="late_four", bufs=4))
+        for j in range(0, CHUNKS + 2):
+            period(j)

@@ -18,6 +18,7 @@ D = 1024
 K = 2048
 PACK = 4
 HALVES = S // PACK
+PAIRS = S // 2
 KT = 128
 WIDTHS = (2, 2, 2, 2, 2, 2, 2, 1, 1)
 CHUNKS = len(WIDTHS)
@@ -26,9 +27,42 @@ KC = KT * TILES
 CE = KC * S
 DT = 512
 BANKS = D // DT
+ON_TENSOR = 2
+V2_IN_PSUM = True
 
 FLOPS = 2 * (2 * P * S * K * D) + 2 * P * K * D
 BYTES = 2 * (P * S * D + P * D + K * D + P * S * K) + 4 * (2 * P * K * S + P * K + K * D)
+
+PATTERN = (
+    ("load_np2", 3),
+    ("load_g", 3),
+    ("load_dot", 1),
+    ("load_w", -1),
+    ("root_u", 2),
+    ("square_u", 1),
+    ("roots_q", 3),
+    ("turn_back", -1),
+    ("add_terms", -2),
+    ("scale_on_gpsimd", -2),
+    ("sum_late", -1),
+    ("over_nq2_late", -1),
+    ("products_mx", -1),
+    ("times_v", 1),
+    ("scale_on_vector", -2),
+    ("v2_to_psum", 2),
+    ("third_a", -1),
+    ("times_dot", 0),
+    ("sum_on_tensor", 0),
+    ("copy_sums", 0),
+    ("third_b", -1),
+    ("sum_early", 0),
+    ("times_u", 1),
+    ("round_g_dot", 1),
+    ("over_nq2_early", 0),
+    ("third_early", 0),
+    ("over_np2", 0),
+    ("quantize", 0),
+)
 
 BANDS = ((0, 4, 32), (64, 2, 0), (96, 2, 96))
 
@@ -55,6 +89,8 @@ def tile_mpl_v_kernel(tc, p, q, W, dot, np2, nq2, grad_out, out):
     ce = [KT * n * S for n in WIDTHS]
     ks = [slice(KT * tile0[i], KT * tile0[i] + kc[i]) for i in range(CHUNKS)]
     es = [slice(KT * tile0[i] * S, KT * tile0[i] * S + ce[i]) for i in range(CHUNKS)]
+    on_tensor = [min(ON_TENSOR, n) if n == TILES else 0 for n in WIDTHS]
+    early = [n == 0 for n in on_tensor]
 
     def live(i):
         return 0 <= i < CHUNKS
@@ -68,8 +104,8 @@ def tile_mpl_v_kernel(tc, p, q, W, dot, np2, nq2, grad_out, out):
         three = ctx.enter_context(tc.tile_pool(name="three", bufs=3))
         two = ctx.enter_context(tc.tile_pool(name="two", bufs=2))
         psum_mx = ctx.enter_context(tc.psum_pool(name="psum_mx", bufs=4))
-        psum_third = ctx.enter_context(tc.psum_pool(name="psum_third", bufs=3))
-        psum_sums = ctx.enter_context(tc.psum_pool(name="psum_sums", bufs=1))
+        psum_third = ctx.enter_context(tc.psum_pool(name="psum_third", bufs=2))
+        psum_one = ctx.enter_context(tc.psum_pool(name="psum_one", bufs=1))
 
         ident = keep.tile([P, P], F32)
         make_identity(nc, ident[:])
@@ -82,12 +118,6 @@ def tile_mpl_v_kernel(tc, p, q, W, dot, np2, nq2, grad_out, out):
         st = [{} for i in range(CHUNKS)]
         late = {}
 
-        def grouped_view(ap):
-            return ap.rearrange("b (h k j) -> b k h j", h=HALVES, j=PACK)
-
-        def natural_view(ap):
-            return ap.rearrange("b (k h j) -> b k h j", h=HALVES, j=PACK)
-
         def load_np2(i):
             u_t = three.tile([P, CE], F32, name="u_t")
             load_by_batch(nc, u_t[:, : ce[i]], np2_flat[:, es[i]])
@@ -99,16 +129,17 @@ def tile_mpl_v_kernel(tc, p, q, W, dot, np2, nq2, grad_out, out):
             st[i]["g"] = g_t[:, : ce[i]]
 
         def load_dot(i):
-            hd_t = three.tile([P, CE], F32, name="hd_t")
-            load_by_batch(nc, hd_t[:, : ce[i]], dot_flat[:, es[i]])
-            st[i]["hd"] = hd_t[:, : ce[i]]
+            dot_t = two.tile([P, CE], F32, name="dot_t")
+            load_by_batch(nc, dot_t[:, : ce[i]], dot_flat[:, es[i]])
+            st[i]["dot"] = dot_t[:, : ce[i]]
 
         def load_w(i):
             w_t = late["two"].tile([P, TILES, D], BF16, name="w_t")
             nc.sync.dma_start(out=w_t[:, : WIDTHS[i], :], in_=w_tiles[:, tile0[i] : tile0[i] + WIDTHS[i], :])
             st[i]["w"] = w_t
 
-        def roots_q(cols):
+        def roots_q(i):
+            cols = ks[i]
             nc.scalar.activation(
                 out=v2_all[:, cols], in_=v2_all[:, cols], func=ACT.Abs_reciprocal_sqrt, scale=float(2 ** 18)
             )
@@ -125,21 +156,27 @@ def tile_mpl_v_kernel(tc, p, q, W, dot, np2, nq2, grad_out, out):
         def round_g_dot(i):
             ab_t = two.tile([P, 2, CE], BF16, name="ab_t", align_bytes=64)
             nc.scalar.activation(
-                out=grouped_view(ab_t[:, 0, : ce[i]]), in_=natural_view(st[i]["a"]), func=ACT.Copy, scale=-0.5
+                out=ab_t[:, 0, : ce[i]].rearrange("b (h k j) -> b k h j", h=HALVES, j=PACK),
+                in_=st[i]["a"].rearrange("b (k h j) -> b k h j", h=HALVES, j=PACK),
+                func=ACT.Copy,
+                scale=-0.5,
             )
             st[i]["ab"] = ab_t
 
         def copy_sums(i):
+            if on_tensor[i] == 0:
+                return
             sums_sb = two.tile([P, KC], F32, name="sums_sb")
-            nc.scalar.copy(out=sums_sb[:, : kc[i]], in_=st[i]["sums"][:, : kc[i]])
+            nc.scalar.copy(out=sums_sb[:, : KT * on_tensor[i]], in_=st[i]["sums"][:, : KT * on_tensor[i]])
             st[i]["sums_sb"] = sums_sb
 
         def times_v(i):
             a_t = two.tile([P, CE], F32, name="a_t")
+            v2 = st[i]["v2p"][:, : kc[i]] if V2_IN_PSUM else v2_all[:, ks[i]]
             nc.vector.tensor_tensor(
                 out=a_t[:, : ce[i]].rearrange("b (k s) -> b k s", s=S),
                 in0=st[i]["g"].rearrange("b (k s) -> b k s", s=S),
-                in1=v2_all[:, ks[i]].unsqueeze(2).to_broadcast([P, kc[i], S]),
+                in1=v2.unsqueeze(2).to_broadcast([P, kc[i], S]),
                 op=ALU.mult,
             )
             st[i]["a"] = a_t[:, : ce[i]]
@@ -148,22 +185,51 @@ def tile_mpl_v_kernel(tc, p, q, W, dot, np2, nq2, grad_out, out):
             nc.vector.tensor_tensor(out=st[i]["a"], in0=st[i]["a"], in1=st[i]["u"], op=ALU.mult)
 
         def times_dot(i):
-            nc.vector.tensor_tensor(out=st[i]["hd"], in0=st[i]["a"], in1=st[i]["hd"], op=ALU.mult)
+            hd_t = two.tile([P, CE], F32, name="hd_t")
+            hd = hd_t[:, : ce[i]].rearrange("b (m k e) -> b k m e", m=PAIRS, e=2)
+            nc.vector.tensor_tensor(
+                out=hd,
+                in0=st[i]["a"].rearrange("b (k m e) -> b k m e", m=PAIRS, e=2),
+                in1=st[i]["dot"].rearrange("b (k m e) -> b k m e", m=PAIRS, e=2),
+                op=ALU.mult,
+            )
+            st[i]["hd"] = hd
+            st[i]["hd_flat"] = hd_t
+
+        def sum_on_vector(i):
+            n = on_tensor[i]
+            if n == WIDTHS[i]:
+                return
+            hs_t = two.tile([P, KC], F32, name="hs_t")
+            nc.vector.tensor_reduce(
+                out=hs_t[:, KT * n : kc[i]], in_=st[i]["hd"][:, KT * n : kc[i]], axis=mybir.AxisListType.XY, op=ALU.add
+            )
+            st[i]["hs"] = hs_t
 
         def over_nq2(i):
             gq_t = two.tile([P, KC], F32, name="gq_t")
-            nc.vector.tensor_tensor(
-                out=gq_t[:, : kc[i]], in0=st[i]["sums"][:, KC : KC + kc[i]], in1=inq_all[:, ks[i]], op=ALU.mult
-            )
+            n = KT * on_tensor[i]
+            k0 = KT * tile0[i]
+            if n > 0:
+                nc.vector.tensor_tensor(
+                    out=gq_t[:, :n], in0=st[i]["sums"][:, KC : KC + n], in1=inq_all[:, k0 : k0 + n], op=ALU.mult
+                )
+            if n < kc[i]:
+                nc.vector.tensor_tensor(
+                    out=gq_t[:, n : kc[i]], in0=st[i]["hs"][:, n : kc[i]], in1=inq_all[:, k0 + n : k0 + kc[i]], op=ALU.mult
+                )
             st[i]["gq"] = gq_t
 
         def over_np2(i):
-            nc.vector.tensor_tensor(
-                out=grouped_view(st[i]["ab"][:, 1, : ce[i]]),
-                in0=natural_view(st[i]["hd"]),
-                in1=natural_view(st[i]["w4"]),
-                op=ALU.mult,
-            )
+            for h in range(HALVES):
+                nc.vector.tensor_tensor(
+                    out=st[i]["ab"][:, 1, h * kc[i] * PACK : (h + 1) * kc[i] * PACK].rearrange(
+                        "b (k m e) -> b k m e", m=2, e=2
+                    ),
+                    in0=st[i]["hd"][:, :, 2 * h : 2 * h + 2, :],
+                    in1=st[i]["w4"].rearrange("b (k m e) -> b k m e", m=PAIRS, e=2)[:, :, 2 * h : 2 * h + 2, :],
+                    op=ALU.mult,
+                )
 
         def quantize(i):
             a_codes = two.tile([P, 2, HALVES * KC], U32, name="a_codes", align_bytes=64)
@@ -187,23 +253,49 @@ def tile_mpl_v_kernel(tc, p, q, W, dot, np2, nq2, grad_out, out):
                         op0=ALU.mult, op1=ALU.add,
                     )
 
-        def scale_and_store(i):
-            for t in range(WIDTHS[i]):
-                out_t = st[i]["out"][t]
-                for c in range(BANKS):
-                    nc.gpsimd.tensor_tensor(
-                        out=out_t[:, banks[c]], in0=out_t[:, banks[c]], in1=st[i]["w"][:, t, banks[c]], op=ALU.mult
-                    )
-                row0 = (tile0[i] + t) * KT
-                nc.sync.dma_start(out=out[row0 : row0 + KT, :], in_=out_t[:])
+        def times_w(engine, i, t, c):
+            out_t = st[i]["out"][t]
+            engine.tensor_tensor(
+                out=out_t[:, banks[c]], in0=out_t[:, banks[c]], in1=st[i]["w"][:, t, banks[c]], op=ALU.mult
+            )
 
-        def sum_over_s(i):
-            sums = psum_sums.tile([P, 2 * KC], F32, name="sums")
-            for t in range(WIDTHS[i]):
+        def store(i, t):
+            row0 = (tile0[i] + t) * KT
+            nc.sync.dma_start(out=out[row0 : row0 + KT, :], in_=st[i]["out"][t][:])
+
+        def vector_share(i):
+            return units(i)[len(units(i)) - (1 if i < CHUNKS - 1 else len(units(i))) :]
+
+        def scale_on_gpsimd(i):
+            for t, c in units(i):
+                if (t, c) not in vector_share(i):
+                    times_w(nc.gpsimd, i, t, c)
+                    if c == BANKS - 1:
+                        store(i, t)
+
+        def scale_on_vector(i):
+            for t, c in vector_share(i):
+                times_w(nc.vector, i, t, c)
+                if c == BANKS - 1:
+                    store(i, t)
+
+        def v2_to_psum(i):
+            if not V2_IN_PSUM:
+                return
+            v2p = psum_one.tile([P, KC], F32, name="v2p")
+            nc.tensor.matmul(out=v2p[:, : kc[i]], lhsT=ident[:], rhs=v2_all[:, ks[i]], start=True, stop=True)
+            st[i]["v2p"] = v2p
+
+        def sum_on_tensor(i):
+            if on_tensor[i] == 0:
+                return
+            sums = psum_one.tile([P, 2 * KC], F32, name="sums")
+            for t in range(on_tensor[i]):
                 for s in range(S):
+                    first = (s // 2) * kc[i] * 2 + t * KT * 2 + s % 2
                     nc.tensor.matmul(
                         out=sums[:, rows[t]],
-                        lhsT=st[i]["hd"][:, t * KT * S + s : (t + 1) * KT * S : S],
+                        lhsT=st[i]["hd_flat"][:, first : first + 2 * KT - 1 : 2],
                         rhs=ident[:],
                         is_transpose=True,
                         start=(s == 0),
@@ -212,7 +304,7 @@ def tile_mpl_v_kernel(tc, p, q, W, dot, np2, nq2, grad_out, out):
             st[i]["sums"] = sums
 
         def turn_back(i):
-            for t in range(WIDTHS[i]):
+            for t in range(on_tensor[i]):
                 nc.tensor.transpose(st[i]["sums"][:, KC + t * KT : KC + (t + 1) * KT], st[i]["sums_sb"][:, rows[t]], ident[:])
 
         def products_mx(i):
@@ -233,9 +325,11 @@ def tile_mpl_v_kernel(tc, p, q, W, dot, np2, nq2, grad_out, out):
                         )
                 st[i]["mx"][(t, c)] = mx_ps
 
-        def products_third(i):
-            st[i]["third"] = {}
-            for t, c in units(i):
+        def products_third(i, part):
+            if part == 0:
+                st[i]["third"] = {}
+            half = len(units(i)) // 2
+            for t, c in units(i)[part * half : (part + 1) * half]:
                 third_ps = psum_third.tile([KT, DT], F32, name="third_ps")
                 nc.tensor.matmul(
                     out=third_ps[:], lhsT=st[i]["gq"][:, rows[t]], rhs=ql2[:, banks[c]], start=True, stop=True
@@ -244,39 +338,23 @@ def tile_mpl_v_kernel(tc, p, q, W, dot, np2, nq2, grad_out, out):
                 nc.scalar.activation(out=third_sb[:], in_=third_ps[:], func=ACT.Copy, scale=2.0)
                 st[i]["third"][(t, c)] = third_sb
 
+        steps = {
+            "load_np2": load_np2, "load_g": load_g, "load_dot": load_dot, "load_w": load_w,
+            "copy_sums": copy_sums, "root_u": root_u, "square_u": square_u, "round_g_dot": round_g_dot,
+            "add_terms": add_terms, "sum_on_vector": sum_on_vector, "times_v": times_v, "over_nq2": over_nq2,
+            "times_dot": times_dot, "times_u": times_u, "over_np2": over_np2, "quantize": quantize,
+            "scale_on_gpsimd": scale_on_gpsimd, "scale_on_vector": scale_on_vector, "turn_back": turn_back, "products_mx": products_mx, "roots_q": roots_q,
+            "v2_to_psum": v2_to_psum, "sum_on_tensor": sum_on_tensor,
+            "third_a": lambda i: early[i] or products_third(i, 0), "third_b": lambda i: early[i] or products_third(i, 1),
+            "third_early": lambda i: early[i] and (products_third(i, 0), products_third(i, 1)),
+            "sum_late": lambda i: early[i] or sum_on_vector(i), "sum_early": lambda i: early[i] and sum_on_vector(i),
+            "over_nq2_late": lambda i: early[i] or over_nq2(i), "over_nq2_early": lambda i: early[i] and over_nq2(i),
+        }
+
         def period(j):
-            if live(j + 3):
-                load_np2(j + 3)
-                load_g(j + 3)
-            if live(j + 2):
-                load_dot(j + 2)
-            if live(j - 1):
-                load_w(j - 1)
-            if live(j + 2):
-                root_u(j + 2)
-            if live(j + 1):
-                square_u(j + 1)
-            if live(j - 1):
-                turn_back(j - 1)
-            if live(j - 2):
-                add_terms(j - 2)
-                scale_and_store(j - 2)
-            if live(j - 1):
-                products_mx(j - 1)
-                over_nq2(j - 1)
-                products_third(j - 1)
-            if live(j + 1):
-                times_v(j + 1)
-            if live(j):
-                times_dot(j)
-                sum_over_s(j)
-            if live(j + 1):
-                times_u(j + 1)
-                round_g_dot(j + 1)
-            if live(j):
-                over_np2(j)
-                quantize(j)
-                copy_sums(j)
+            for name, ahead in PATTERN:
+                if live(j + ahead):
+                    steps[name](j + ahead)
 
         load_by_batch(nc, ql, q[:, S - 1, :])
         with tc.tile_pool(name="xonce", bufs=1) as xonce, tc.tile_pool(name="xwork", bufs=2) as xwork:
@@ -294,7 +372,6 @@ def tile_mpl_v_kernel(tc, p, q, W, dot, np2, nq2, grad_out, out):
             load_g(1)
             load_np2(1)
             load_by_batch(nc, v2_all[:, 2 * KC :], nq2[:, 2 * KC :])
-            load_dot(1)
             load_g(2)
             load_np2(2)
             grouped = {}
@@ -315,9 +392,12 @@ def tile_mpl_v_kernel(tc, p, q, W, dot, np2, nq2, grad_out, out):
                 )
                 grouped[h] = (x1g, x2g)
                 if h == 0:
-                    roots_q(slice(0, 2 * KC))
+                    roots_q(0)
+                    roots_q(1)
                     root_u(0)
+            v2_to_psum(0)
             times_v(0)
+            v2_to_psum(1)
             for h in range(HALVES):
                 nc.vector.quantize_mx(
                     out=x_codes[:, 0, h, :].bitcast(E4M3X4),
@@ -334,8 +414,8 @@ def tile_mpl_v_kernel(tc, p, q, W, dot, np2, nq2, grad_out, out):
                 )
             square_u(0)
             root_u(1)
+            roots_q(2)
             nc.scalar.activation(out=ql2[:], in_=ql[:], func=ACT.Square)
-            roots_q(slice(2 * KC, K))
 
         late["two"] = ctx.enter_context(tc.tile_pool(name="late_two", bufs=2))
         late["four"] = ctx.enter_context(tc.tile_pool(name="late_four", bufs=4))

@@ -27,6 +27,7 @@ KC = KT * TILES
 CE = KC * S
 DT = 512
 BANKS = D // DT
+NQ_FIRST = 4 * KC
 ON_TENSOR = 2
 V2_IN_PSUM = True
 
@@ -34,11 +35,12 @@ FLOPS = 2 * (2 * P * S * K * D) + 2 * P * K * D
 BYTES = 2 * (P * S * D + P * D + K * D + P * S * K) + 4 * (2 * P * K * S + P * K + K * D)
 
 PATTERN = (
-    ("load_np2", 3),
-    ("load_g", 3),
+    ("load_np2", 2),
+    ("load_g", 2),
     ("load_dot", 1),
+    ("load_nq2_rest", 2),
     ("load_w", -1),
-    ("root_u", 2),
+    ("root_u", 1),
     ("square_u", 1),
     ("roots_q", 3),
     ("turn_back", -1),
@@ -339,6 +341,7 @@ def tile_mpl_v_kernel(tc, p, q, W, dot, np2, nq2, grad_out, out):
                 st[i]["third"][(t, c)] = third_sb
 
         steps = {
+            "load_nq2_rest": lambda i: i == 2 and load_by_batch(nc, v2_all[:, NQ_FIRST:], nq2[:, NQ_FIRST:]),
             "load_np2": load_np2, "load_g": load_g, "load_dot": load_dot, "load_w": load_w,
             "copy_sums": copy_sums, "root_u": root_u, "square_u": square_u, "round_g_dot": round_g_dot,
             "add_terms": add_terms, "sum_on_vector": sum_on_vector, "times_v": times_v, "over_nq2": over_nq2,
@@ -365,17 +368,15 @@ def tile_mpl_v_kernel(tc, p, q, W, dot, np2, nq2, grad_out, out):
                     p_t[:, PACK * h : PACK * (h + 1), :].rearrange("b s d -> b (s d)"),
                     p[:, PACK * h : PACK * (h + 1), :].rearrange("b s d -> b (s d)"),
                 )
-            load_by_batch(nc, v2_all[:, : 2 * KC], nq2[:, : 2 * KC])
+            load_by_batch(nc, v2_all[:, : NQ_FIRST], nq2[:, : NQ_FIRST])
             load_g(0)
             load_np2(0)
-            load_dot(0)
             load_g(1)
+            load_dot(0)
             load_np2(1)
-            load_by_batch(nc, v2_all[:, 2 * KC :], nq2[:, 2 * KC :])
-            load_g(2)
-            load_np2(2)
             grouped = {}
-            for h in range(HALVES):
+
+            def products_of_p(h):
                 p_rows = p_t[:, PACK * h : PACK * (h + 1), :]
                 x1g = xwork.tile([P, D, PACK], BF16, name="x1g", align_bytes=64)
                 nc.vector.tensor_tensor(
@@ -391,31 +392,30 @@ def tile_mpl_v_kernel(tc, p, q, W, dot, np2, nq2, grad_out, out):
                     func=ACT.Square,
                 )
                 grouped[h] = (x1g, x2g)
-                if h == 0:
-                    roots_q(0)
-                    roots_q(1)
-                    root_u(0)
+
+            def quantize_x(o):
+                for h in range(HALVES):
+                    nc.vector.quantize_mx(
+                        out=x_codes[:, o, h, :].bitcast(E4M3X4),
+                        scales=x_scales[:, o, h, :],
+                        in_=grouped[h][o][:].rearrange("b d j -> b (d j)"),
+                    )
+
+            products_of_p(0)
+            roots_q(0)
+            roots_q(1)
             v2_to_psum(0)
+            nc.scalar.activation(out=ql2[:], in_=ql[:], func=ACT.Square)
+            roots_q(2)
+            root_u(0)
+            products_of_p(1)
             times_v(0)
             v2_to_psum(1)
-            for h in range(HALVES):
-                nc.vector.quantize_mx(
-                    out=x_codes[:, 0, h, :].bitcast(E4M3X4),
-                    scales=x_scales[:, 0, h, :],
-                    in_=grouped[h][0][:].rearrange("b d j -> b (d j)"),
-                )
+            quantize_x(0)
             times_u(0)
             round_g_dot(0)
-            for h in range(HALVES):
-                nc.vector.quantize_mx(
-                    out=x_codes[:, 1, h, :].bitcast(E4M3X4),
-                    scales=x_scales[:, 1, h, :],
-                    in_=grouped[h][1][:].rearrange("b d j -> b (d j)"),
-                )
+            quantize_x(1)
             square_u(0)
-            root_u(1)
-            roots_q(2)
-            nc.scalar.activation(out=ql2[:], in_=ql[:], func=ACT.Square)
 
         late["two"] = ctx.enter_context(tc.tile_pool(name="late_two", bufs=2))
         late["four"] = ctx.enter_context(tc.tile_pool(name="late_four", bufs=4))

@@ -39,7 +39,8 @@ PATTERN = (
     ("load_g", 2),
     ("load_dot", 1),
     ("load_nq2_rest", 2),
-    ("load_w", -1),
+    ("load_w", 0),
+    ("store_out", -4),
     ("root_u", 1),
     ("square_u", 1),
     ("roots_q", 3),
@@ -64,6 +65,21 @@ PATTERN = (
     ("third_early", 0),
     ("over_np2", 0),
     ("quantize", 0),
+)
+
+LAST_PATTERN = (
+    ("load_w", 0),
+    ("store_out", -4),
+    ("times_dot", 0),
+    ("products_mx", -1),
+    ("sum_early", 0),
+    ("over_np2", 0),
+    ("over_nq2_early", 0),
+    ("third_early", 0),
+    ("quantize", 0),
+    ("add_terms", -2),
+    ("scale_on_gpsimd", -2),
+    ("scale_on_vector", -2),
 )
 
 BANDS = ((0, 4, 32), (64, 2, 0), (96, 2, 96))
@@ -136,7 +152,7 @@ def tile_mpl_v_kernel(tc, p, q, W, dot, np2, nq2, grad_out, out):
             st[i]["dot"] = dot_t[:, : ce[i]]
 
         def load_w(i):
-            w_t = late["two"].tile([P, TILES, D], BF16, name="w_t")
+            w_t = late["four"].tile([P, TILES, D], BF16, name="w_t")
             nc.sync.dma_start(out=w_t[:, : WIDTHS[i], :], in_=w_tiles[:, tile0[i] : tile0[i] + WIDTHS[i], :])
             st[i]["w"] = w_t
 
@@ -247,7 +263,7 @@ def tile_mpl_v_kernel(tc, p, q, W, dot, np2, nq2, grad_out, out):
         def add_terms(i):
             st[i]["out"] = []
             for t in range(WIDTHS[i]):
-                out_t = late["four"].tile([P, D], F32, name="out_t")
+                out_t = late["out"].tile([P, D], F32, name="out_t")
                 st[i]["out"].append(out_t)
                 for c in range(BANKS):
                     nc.vector.scalar_tensor_tensor(
@@ -266,20 +282,25 @@ def tile_mpl_v_kernel(tc, p, q, W, dot, np2, nq2, grad_out, out):
             nc.sync.dma_start(out=out[row0 : row0 + KT, :], in_=st[i]["out"][t][:])
 
         def vector_share(i):
-            return units(i)[len(units(i)) - (1 if i < CHUNKS - 1 else len(units(i))) :]
+            return units(i)[len(units(i)) - (1 if i < CHUNKS - 2 else len(units(i))) :]
 
         def scale_on_gpsimd(i):
             for t, c in units(i):
                 if (t, c) not in vector_share(i):
                     times_w(nc.gpsimd, i, t, c)
-                    if c == BANKS - 1:
-                        store(i, t)
 
         def scale_on_vector(i):
             for t, c in vector_share(i):
                 times_w(nc.vector, i, t, c)
-                if c == BANKS - 1:
+
+        def store_out(i):
+            for t in range(WIDTHS[i]):
+                if i < CHUNKS - 1:
                     store(i, t)
+                else:
+                    row0 = (tile0[i] + t) * KT
+                    for c in range(BANKS):
+                        nc.sync.dma_start(out=out[row0 : row0 + KT, banks[c]], in_=st[i]["out"][t][:, banks[c]])
 
         def v2_to_psum(i):
             if not V2_IN_PSUM:
@@ -346,7 +367,7 @@ def tile_mpl_v_kernel(tc, p, q, W, dot, np2, nq2, grad_out, out):
             "copy_sums": copy_sums, "root_u": root_u, "square_u": square_u, "round_g_dot": round_g_dot,
             "add_terms": add_terms, "sum_on_vector": sum_on_vector, "times_v": times_v, "over_nq2": over_nq2,
             "times_dot": times_dot, "times_u": times_u, "over_np2": over_np2, "quantize": quantize,
-            "scale_on_gpsimd": scale_on_gpsimd, "scale_on_vector": scale_on_vector, "turn_back": turn_back, "products_mx": products_mx, "roots_q": roots_q,
+            "store_out": store_out, "scale_on_gpsimd": scale_on_gpsimd, "scale_on_vector": scale_on_vector, "turn_back": turn_back, "products_mx": products_mx, "roots_q": roots_q,
             "v2_to_psum": v2_to_psum, "sum_on_tensor": sum_on_tensor,
             "third_a": lambda i: early[i] or products_third(i, 0), "third_b": lambda i: early[i] or products_third(i, 1),
             "third_early": lambda i: early[i] and (products_third(i, 0), products_third(i, 1)),
@@ -355,7 +376,7 @@ def tile_mpl_v_kernel(tc, p, q, W, dot, np2, nq2, grad_out, out):
         }
 
         def period(j):
-            for name, ahead in PATTERN:
+            for name, ahead in (LAST_PATTERN if j == CHUNKS - 1 else PATTERN):
                 if live(j + ahead):
                     steps[name](j + ahead)
 
@@ -419,5 +440,6 @@ def tile_mpl_v_kernel(tc, p, q, W, dot, np2, nq2, grad_out, out):
 
         late["two"] = ctx.enter_context(tc.tile_pool(name="late_two", bufs=2))
         late["four"] = ctx.enter_context(tc.tile_pool(name="late_four", bufs=4))
-        for j in range(0, CHUNKS + 2):
+        late["out"] = ctx.enter_context(tc.tile_pool(name="late_out", bufs=8))
+        for j in range(0, CHUNKS + 5):
             period(j)

@@ -282,7 +282,7 @@ def tile_mpl_v_kernel(tc, p, q, W, dot, np2, nq2, grad_out, out):
             nc.sync.dma_start(out=out[row0 : row0 + KT, :], in_=st[i]["out"][t][:])
 
         def vector_share(i):
-            return units(i)[len(units(i)) - (1 if i < CHUNKS - 2 else len(units(i))) :]
+            return units(i)[len(units(i)) - (0 if i < CHUNKS - 2 else len(units(i))) :]
 
         def scale_on_gpsimd(i):
             for t, c in units(i):

from contextlib import ExitStack

import concourse.mybir as mybir
from concourse.masks import make_identity

F32 = mybir.dt.float32
BF16 = mybir.dt.bfloat16
U32 = mybir.dt.uint32
U8 = mybir.dt.uint8
E4M3X4 = mybir.dt.float8_e4m3fn_x4
E5M2X4 = mybir.dt.float8_e5m2_x4
ACT = mybir.ActivationFunctionType
ALU = mybir.AluOpType

P = 128
S = 8
D = 1024
K = 2048
PACK = 4
HALVES = S // PACK
PAIRS = S // 2
KT = 128
WIDTHS = (2, 2, 2, 2, 2, 2, 2, 1, 1)
CHUNKS = len(WIDTHS)
TILES = max(WIDTHS)
KC = KT * TILES
CE = KC * S
DT = 512
BANKS = D // DT
NQ_FIRST = 4 * KC
ON_TENSOR = 2
V2_IN_PSUM = True

FLOPS = 2 * (2 * P * S * K * D) + 2 * P * K * D
BYTES = 2 * (P * S * D + P * D + K * D + P * S * K) + 4 * (2 * P * K * S + P * K + K * D)

PATTERN = (
    ("load_np2", 2),
    ("load_g", 2),
    ("load_dot", 1),
    ("load_nq2_rest", 2),
    ("load_w", 0),
    ("store_out", -4),
    ("root_u", 1),
    ("square_u", 1),
    ("roots_q", 3),
    ("turn_back", -1),
    ("add_terms", -2),
    ("scale_on_gpsimd", -2),
    ("sum_late", -1),
    ("over_nq2_late", -1),
    ("products_mx", -1),
    ("times_v", 1),
    ("scale_on_vector", -2),
    ("v2_to_psum", 2),
    ("third_a", -1),
    ("times_dot", 0),
    ("sum_on_tensor", 0),
    ("copy_sums", 0),
    ("third_b", -1),
    ("sum_early", 0),
    ("times_u", 1),
    ("round_g_dot", 1),
    ("over_nq2_early", 0),
    ("third_early", 0),
    ("over_np2", 0),
    ("quantize", 0),
)

LAST_PATTERN = (
    ("load_w", 0),
    ("store_out", -4),
    ("times_dot", 0),
    ("products_mx", -1),
    ("sum_early", 0),
    ("over_np2", 0),
    ("over_nq2_early", 0),
    ("third_early", 0),
    ("quantize", 0),
    ("add_terms", -2),
    ("scale_on_gpsimd", -2),
    ("scale_on_vector", -2),
)

BANDS = ((0, 4, 32), (64, 2, 0), (96, 2, 96))


def load_by_batch(nc, dst, src):
    for first_batch, repeats, first_partition in BANDS:
        rows = 16 * repeats
        nc.sync.dma_start(
            out=dst[first_partition : first_partition + rows, :],
            in_=src[first_batch : first_batch + rows, :].rearrange("(u r) f -> r u f", r=16),
        )


def tile_mpl_v_kernel(tc, p, q, W, dot, np2, nq2, grad_out, out):
    nc = tc.nc
    g_flat = grad_out.rearrange("b s k -> b (s k)")
    dot_flat = dot.rearrange("b k s -> b (k s)")
    np2_flat = np2.rearrange("b k s -> b (k s)")
    w_tiles = W.rearrange("(t r) d -> r t d", r=KT)
    rows = [slice(t * KT, (t + 1) * KT) for t in range(TILES)]
    banks = [slice(c * DT, (c + 1) * DT) for c in range(BANKS)]
    tile0 = [sum(WIDTHS[:i]) for i in range(CHUNKS)]
    kc = [KT * n for n in WIDTHS]
    ce = [KT * n * S for n in WIDTHS]
    ks = [slice(KT * tile0[i], KT * tile0[i] + kc[i]) for i in range(CHUNKS)]
    es = [slice(KT * tile0[i] * S, KT * tile0[i] * S + ce[i]) for i in range(CHUNKS)]
    on_tensor = [min(ON_TENSOR, n) if n == TILES else 0 for n in WIDTHS]
    early = [n == 0 for n in on_tensor]

    def live(i):
        return 0 <= i < CHUNKS

    def units(i):
        return [(t, c) for t in range(WIDTHS[i]) for c in range(BANKS)]

    with ExitStack() as ctx:
        ctx.enter_context(tc.manual_schedule())
        keep = ctx.enter_context(tc.tile_pool(name="keep", bufs=1))
        three = ctx.enter_context(tc.tile_pool(name="three", bufs=3))
        two = ctx.enter_context(tc.tile_pool(name="two", bufs=2))
        psum_mx = ctx.enter_context(tc.psum_pool(name="psum_mx", bufs=4))
        psum_third = ctx.enter_context(tc.psum_pool(name="psum_third", bufs=2))
        psum_one = ctx.enter_context(tc.psum_pool(name="psum_one", bufs=1))

        ident = keep.tile([P, P], F32)
        make_identity(nc, ident[:])
        ql = keep.tile([P, D], BF16)
        ql2 = keep.tile([P, D], F32)
        v2_all = keep.tile([P, K], F32)
        inq_all = keep.tile([P, K], F32)
        x_codes = keep.tile([P, 2, HALVES, D], U32, align_bytes=64)
        x_scales = keep.tile([P, 2, HALVES, D], U8, align_bytes=64)
        st = [{} for i in range(CHUNKS)]
        late = {}

        def load_np2(i):
            u_t = three.tile([P, CE], F32, name="u_t")
            load_by_batch(nc, u_t[:, : ce[i]], np2_flat[:, es[i]])
            st[i]["u"] = u_t[:, : ce[i]]

        def load_g(i):
            g_t = three.tile([P, CE], BF16, name="g_t")
            load_by_batch(nc, g_t[:, : ce[i]], g_flat[:, es[i]])
            st[i]["g"] = g_t[:, : ce[i]]

        def load_dot(i):
            dot_t = two.tile([P, CE], F32, name="dot_t")
            load_by_batch(nc, dot_t[:, : ce[i]], dot_flat[:, es[i]])
            st[i]["dot"] = dot_t[:, : ce[i]]

        def load_w(i):
            w_t = late["four"].tile([P, TILES, D], BF16, name="w_t")
            nc.sync.dma_start(out=w_t[:, : WIDTHS[i], :], in_=w_tiles[:, tile0[i] : tile0[i] + WIDTHS[i], :])
            st[i]["w"] = w_t

        def roots_q(i):
            cols = ks[i]
            nc.scalar.activation(
                out=v2_all[:, cols], in_=v2_all[:, cols], func=ACT.Abs_reciprocal_sqrt, scale=float(2 ** 18)
            )
            nc.scalar.activation(out=inq_all[:, cols], in_=v2_all[:, cols], func=ACT.Square, scale=256.0)

        def root_u(i):
            nc.scalar.activation(out=st[i]["u"], in_=st[i]["u"], func=ACT.Abs_reciprocal_sqrt)

        def square_u(i):
            w4_t = two.tile([P, CE], F32, name="w4_t")
            nc.scalar.activation(out=w4_t[:, : ce[i]], in_=st[i]["u"], func=ACT.Square, scale=0.5)
            st[i]["w4"] = w4_t[:, : ce[i]]

        def round_g_dot(i):
            ab_t = two.tile([P, 2, CE], BF16, name="ab_t", align_bytes=64)
            nc.scalar.activation(
                out=ab_t[:, 0, : ce[i]].rearrange("b (h k j) -> b k h j", h=HALVES, j=PACK),
                in_=st[i]["a"].rearrange("b (k h j) -> b k h j", h=HALVES, j=PACK),
                func=ACT.Copy,
                scale=-0.5,
            )
            st[i]["ab"] = ab_t

        def copy_sums(i):
            if on_tensor[i] == 0:
                return
            sums_sb = two.tile([P, KC], F32, name="sums_sb")
            nc.scalar.copy(out=sums_sb[:, : KT * on_tensor[i]], in_=st[i]["sums"][:, : KT * on_tensor[i]])
            st[i]["sums_sb"] = sums_sb

        def times_v(i):
            a_t = two.tile([P, CE], F32, name="a_t")
            v2 = st[i]["v2p"][:, : kc[i]] if V2_IN_PSUM else v2_all[:, ks[i]]
            nc.vector.tensor_tensor(
                out=a_t[:, : ce[i]].rearrange("b (k s) -> b k s", s=S),
                in0=st[i]["g"].rearrange("b (k s) -> b k s", s=S),
                in1=v2.unsqueeze(2).to_broadcast([P, kc[i], S]),
                op=ALU.mult,
            )
            st[i]["a"] = a_t[:, : ce[i]]

        def times_u(i):
            nc.vector.tensor_tensor(out=st[i]["a"], in0=st[i]["a"], in1=st[i]["u"], op=ALU.mult)

        def times_dot(i):
            hd_t = two.tile([P, CE], F32, name="hd_t")
            hd = hd_t[:, : ce[i]].rearrange("b (m k e) -> b k m e", m=PAIRS, e=2)
            nc.vector.tensor_tensor(
                out=hd,
                in0=st[i]["a"].rearrange("b (k m e) -> b k m e", m=PAIRS, e=2),
                in1=st[i]["dot"].rearrange("b (k m e) -> b k m e", m=PAIRS, e=2),
                op=ALU.mult,
            )
            st[i]["hd"] = hd
            st[i]["hd_flat"] = hd_t

        def sum_on_vector(i):
            n = on_tensor[i]
            if n == WIDTHS[i]:
                return
            hs_t = two.tile([P, KC], F32, name="hs_t")
            nc.vector.tensor_reduce(
                out=hs_t[:, KT * n : kc[i]], in_=st[i]["hd"][:, KT * n : kc[i]], axis=mybir.AxisListType.XY, op=ALU.add
            )
            st[i]["hs"] = hs_t

        def over_nq2(i):
            gq_t = two.tile([P, KC], F32, name="gq_t")
            n = KT * on_tensor[i]
            k0 = KT * tile0[i]
            if n > 0:
                nc.vector.tensor_tensor(
                    out=gq_t[:, :n], in0=st[i]["sums"][:, KC : KC + n], in1=inq_all[:, k0 : k0 + n], op=ALU.mult
                )
            if n < kc[i]:
                nc.vector.tensor_tensor(
                    out=gq_t[:, n : kc[i]], in0=st[i]["hs"][:, n : kc[i]], in1=inq_all[:, k0 + n : k0 + kc[i]], op=ALU.mult
                )
            st[i]["gq"] = gq_t

        def over_np2(i):
            for h in range(HALVES):
                nc.vector.tensor_tensor(
                    out=st[i]["ab"][:, 1, h * kc[i] * PACK : (h + 1) * kc[i] * PACK].rearrange(
                        "b (k m e) -> b k m e", m=2, e=2
                    ),
                    in0=st[i]["hd"][:, :, 2 * h : 2 * h + 2, :],
                    in1=st[i]["w4"].rearrange("b (k m e) -> b k m e", m=PAIRS, e=2)[:, :, 2 * h : 2 * h + 2, :],
                    op=ALU.mult,
                )

        def quantize(i):
            a_codes = two.tile([P, 2, HALVES * KC], U32, name="a_codes", align_bytes=64)
            a_scales = two.tile([P, 2, HALVES * KC], U8, name="a_scales", align_bytes=64)
            for o in range(2):
                nc.vector.quantize_mx(
                    out=a_codes[:, o, : HALVES * kc[i]].bitcast(E5M2X4),
                    scales=a_scales[:, o, : HALVES * kc[i]],
                    in_=st[i]["ab"][:, o, : ce[i]],
                )
            st[i]["codes"], st[i]["scales"] = a_codes, a_scales

        def add_terms(i):
            st[i]["out"] = []
            for t in range(WIDTHS[i]):
                out_t = late["out"].tile([P, D], F32, name="out_t")
                st[i]["out"].append(out_t)
                for c in range(BANKS):
                    nc.vector.scalar_tensor_tensor(
                        out=out_t[:, banks[c]], in0=st[i]["mx"][(t, c)][:], scalar=2.0, in1=st[i]["third"][(t, c)][:],
                        op0=ALU.mult, op1=ALU.add,
                    )

        def times_w(engine, i, t, c):
            out_t = st[i]["out"][t]
            engine.tensor_tensor(
                out=out_t[:, banks[c]], in0=out_t[:, banks[c]], in1=st[i]["w"][:, t, banks[c]], op=ALU.mult
            )

        def store(i, t):
            row0 = (tile0[i] + t) * KT
            nc.sync.dma_start(out=out[row0 : row0 + KT, :], in_=st[i]["out"][t][:])

        def vector_share(i):
            return units(i)[len(units(i)) - (0 if i < CHUNKS - 2 else len(units(i))) :]

        def scale_on_gpsimd(i):
            for t, c in units(i):
                if (t, c) not in vector_share(i):
                    times_w(nc.gpsimd, i, t, c)

        def scale_on_vector(i):
            for t, c in vector_share(i):
                times_w(nc.vector, i, t, c)

        def store_out(i):
            for t in range(WIDTHS[i]):
                if i < CHUNKS - 1:
                    store(i, t)
                else:
                    row0 = (tile0[i] + t) * KT
                    for c in range(BANKS):
                        nc.sync.dma_start(out=out[row0 : row0 + KT, banks[c]], in_=st[i]["out"][t][:, banks[c]])

        def v2_to_psum(i):
            if not V2_IN_PSUM:
                return
            v2p = psum_one.tile([P, KC], F32, name="v2p")
            nc.tensor.matmul(out=v2p[:, : kc[i]], lhsT=ident[:], rhs=v2_all[:, ks[i]], start=True, stop=True)
            st[i]["v2p"] = v2p

        def sum_on_tensor(i):
            if on_tensor[i] == 0:
                return
            sums = psum_one.tile([P, 2 * KC], F32, name="sums")
            for t in range(on_tensor[i]):
                for s in range(S):
                    first = (s // 2) * kc[i] * 2 + t * KT * 2 + s % 2
                    nc.tensor.matmul(
                        out=sums[:, rows[t]],
                        lhsT=st[i]["hd_flat"][:, first : first + 2 * KT - 1 : 2],
                        rhs=ident[:],
                        is_transpose=True,
                        start=(s == 0),
                        stop=(s == S - 1),
                    )
            st[i]["sums"] = sums

        def turn_back(i):
            for t in range(on_tensor[i]):
                nc.tensor.transpose(st[i]["sums"][:, KC + t * KT : KC + (t + 1) * KT], st[i]["sums_sb"][:, rows[t]], ident[:])

        def products_mx(i):
            st[i]["mx"] = {}
            for t, c in units(i):
                mx_ps = psum_mx.tile([KT, DT], F32, name="mx_ps")
                for o in range(2):
                    for h in range(HALVES):
                        cols = slice(h * kc[i] + t * KT, h * kc[i] + (t + 1) * KT)
                        nc.tensor.matmul_mx(
                            out=mx_ps[:],
                            lhsT=st[i]["codes"][:, o, cols].bitcast(E5M2X4),
                            lhsT_scale=st[i]["scales"][:, o, cols],
                            rhs=x_codes[:, o, h, banks[c]].bitcast(E4M3X4),
                            rhs_scale=x_scales[:, o, h, banks[c]],
                            start=(o == 0 and h == 0),
                            stop=(o == 1 and h == HALVES - 1),
                        )
                st[i]["mx"][(t, c)] = mx_ps

        def products_third(i, part):
            if part == 0:
                st[i]["third"] = {}
            half = len(units(i)) // 2
            for t, c in units(i)[part * half : (part + 1) * half]:
                third_ps = psum_third.tile([KT, DT], F32, name="third_ps")
                nc.tensor.matmul(
                    out=third_ps[:], lhsT=st[i]["gq"][:, rows[t]], rhs=ql2[:, banks[c]], start=True, stop=True
                )
                third_sb = late["four"].tile([KT, DT], F32, name="third_sb")
                nc.scalar.activation(out=third_sb[:], in_=third_ps[:], func=ACT.Copy, scale=2.0)
                st[i]["third"][(t, c)] = third_sb

        steps = {
            "load_nq2_rest": lambda i: i == 2 and load_by_batch(nc, v2_all[:, NQ_FIRST:], nq2[:, NQ_FIRST:]),
            "load_np2": load_np2, "load_g": load_g, "load_dot": load_dot, "load_w": load_w,
            "copy_sums": copy_sums, "root_u": root_u, "square_u": square_u, "round_g_dot": round_g_dot,
            "add_terms": add_terms, "sum_on_vector": sum_on_vector, "times_v": times_v, "over_nq2": over_nq2,
            "times_dot": times_dot, "times_u": times_u, "over_np2": over_np2, "quantize": quantize,
            "store_out": store_out, "scale_on_gpsimd": scale_on_gpsimd, "scale_on_vector": scale_on_vector, "turn_back": turn_back, "products_mx": products_mx, "roots_q": roots_q,
            "v2_to_psum": v2_to_psum, "sum_on_tensor": sum_on_tensor,
            "third_a": lambda i: early[i] or products_third(i, 0), "third_b": lambda i: early[i] or products_third(i, 1),
            "third_early": lambda i: early[i] and (products_third(i, 0), products_third(i, 1)),
            "sum_late": lambda i: early[i] or sum_on_vector(i), "sum_early": lambda i: early[i] and sum_on_vector(i),
            "over_nq2_late": lambda i: early[i] or over_nq2(i), "over_nq2_early": lambda i: early[i] and over_nq2(i),
        }

        def period(j):
            for name, ahead in (LAST_PATTERN if j == CHUNKS - 1 else PATTERN):
                if live(j + ahead):
                    steps[name](j + ahead)

        load_by_batch(nc, ql, q[:, S - 1, :])
        with tc.tile_pool(name="xonce", bufs=1) as xonce, tc.tile_pool(name="xwork", bufs=2) as xwork:
            p_t = xonce.tile([P, S, D], BF16)
            for h in range(HALVES):
                load_by_batch(
                    nc,
                    p_t[:, PACK * h : PACK * (h + 1), :].rearrange("b s d -> b (s d)"),
                    p[:, PACK * h : PACK * (h + 1), :].rearrange("b s d -> b (s d)"),
                )
            load_by_batch(nc, v2_all[:, : NQ_FIRST], nq2[:, : NQ_FIRST])
            load_g(0)
            load_np2(0)
            load_g(1)
            load_dot(0)
            load_np2(1)
            grouped = {}

            def products_of_p(h):
                p_rows = p_t[:, PACK * h : PACK * (h + 1), :]
                x1g = xwork.tile([P, D, PACK], BF16, name="x1g", align_bytes=64)
                nc.vector.tensor_tensor(
                    out=x1g[:],
                    in0=p_rows.rearrange("b j d -> b d j"),
                    in1=ql[:].unsqueeze(2).to_broadcast([P, D, PACK]),
                    op=ALU.mult,
                )
                x2g = xwork.tile([P, D, PACK], BF16, name="x2g", align_bytes=64)
                nc.scalar.activation(
                    out=x2g[:].rearrange("b (c i) j -> b c j i", i=4),
                    in_=p_rows.rearrange("b j (c i) -> b c j i", i=4),
                    func=ACT.Square,
                )
                grouped[h] = (x1g, x2g)

            def quantize_x(o):
                for h in range(HALVES):
                    nc.vector.quantize_mx(
                        out=x_codes[:, o, h, :].bitcast(E4M3X4),
                        scales=x_scales[:, o, h, :],
                        in_=grouped[h][o][:].rearrange("b d j -> b (d j)"),
                    )

            products_of_p(0)
            roots_q(0)
            roots_q(1)
            v2_to_psum(0)
            nc.scalar.activation(out=ql2[:], in_=ql[:], func=ACT.Square)
            roots_q(2)
            root_u(0)
            products_of_p(1)
            times_v(0)
            v2_to_psum(1)
            quantize_x(0)
            times_u(0)
            round_g_dot(0)
            quantize_x(1)
            square_u(0)

        late["two"] = ctx.enter_context(tc.tile_pool(name="late_two", bufs=2))
        late["four"] = ctx.enter_context(tc.tile_pool(name="late_four", bufs=4))
        late["out"] = ctx.enter_context(tc.tile_pool(name="late_out", bufs=8))
        for j in range(0, CHUNKS + 5):
            period(j)
